import numpy as np
import ml_dtypes


def mxq(x, axis, fmt="e4m3"):
    dtype, down = {"e4m3": (ml_dtypes.float8_e4m3fn, 7), "e5m2": (ml_dtypes.float8_e5m2, 14)}[fmt]
    v = np.moveaxis(np.asarray(x, np.float32).astype(ml_dtypes.bfloat16).astype(np.float64), axis, -1)
    blocks = v.reshape(v.shape[:-1] + (-1, 32))
    amax = np.abs(blocks).max(-1, keepdims=True)
    byte = np.maximum(np.where(amax > 0, np.frexp(amax)[1] - 1 + 127, 0) - down, 1)
    scale = np.exp2(byte - 127.0)
    codes = (blocks / scale).astype(np.float32).astype(dtype).astype(np.float64)
    return np.moveaxis((codes * scale).reshape(v.shape), -1, axis)


WIDE = False


def mx_kscale(k):
    if not WIDE:
        return np.ones(k)
    levels = np.array([10, -10, 5, -5, 0])
    a = np.random.permutation(np.resize(levels, k // 512 * 4)).reshape(k // 512, 4)
    idx = np.arange(k)
    return np.exp2(a[idx // 512, idx % 128 // 32])


BF16 = ml_dtypes.bfloat16


def bf(x):
    return np.asarray(x, np.float32).astype(BF16)


def f64(x):
    return np.asarray(x).astype(np.float64)


B, S, D, P, N1, N2, N3 = 2, 512, 1024, 128, 3, 2, 3
H = N1 + N2 + N3


def setup_inputs():
    s = mx_kscale(D)
    a = 1.0 / np.sqrt(D)
    return {"x": bf(np.random.standard_normal((B, S, D)) * s),
            "w_now": bf(np.random.standard_normal((H, P, D)) * a / s),
            "w_back1": bf(np.random.standard_normal((N2 + N3, P, D)) * a / s),
            "w_back2": bf(np.random.standard_normal((N3, P, D)) * a / s),
            "bias": bf(np.random.standard_normal((H, P)) * 0.5)}


def reference(x, w_now, w_back1, w_back2, bias):
    xq = mxq(f64(x), 2, "e4m3")
    y = 0.0
    for j, w in enumerate((w_now, w_back1, w_back2)):
        z = xq @ mxq(f64(w), 2, "e4m3").reshape(-1, D).T
        y = y + np.pad(z[:, :S - j], ((0, 0), (j, 0), (H * P - z.shape[-1], 0)))
    return y.reshape(B, S, H, P).transpose(0, 2, 1, 3) + f64(bias)[None, :, None, :]

@@ -1,0 +1,222 @@
+from contextlib import ExitStack
+
+import concourse.mybir as mybir
+from concourse.masks import make_identity
+
+F32 = mybir.dt.float32
+BF16 = mybir.dt.bfloat16
+U32 = mybir.dt.uint32
+U8 = mybir.dt.uint8
+FP8X4 = mybir.dt.float8_e4m3fn_x4
+ADD = mybir.AluOpType.add
+
+B, S, D, P, H = 2, 512, 1024, 128, 8
+R = 4
+G = 2
+FLOPS = 2 * B * S * D * P * 16
+
+
+def tile_multiheadhomogeneousattention_pa_kernel(tc, x, w_now, w_back1, w_back2, bias, out):
+    nc = tc.nc
+    with ExitStack() as ctx:
+        const = ctx.enter_context(tc.tile_pool(name="const", bufs=1))
+        raw = ctx.enter_context(tc.tile_pool(name="raw", bufs=1))
+        grp = ctx.enter_context(tc.tile_pool(name="grp", bufs=1))
+        mxp = ctx.enter_context(tc.tile_pool(name="mxp", bufs=1))
+        outp = ctx.enter_context(tc.tile_pool(name="outp", bufs=1))
+        tpool = ctx.enter_context(tc.psum_pool(name="tpool", bufs=4))
+        apool = ctx.enter_context(tc.psum_pool(name="apool", bufs=4))
+
+        ident = const.tile([P, P], F32, name="ident")
+        make_identity(nc, ident[:])
+        ones = const.tile([P, P], BF16, name="ones")
+        nc.vector.memset(ones[:], 1.0)
+        bias_row = const.tile([P, H * P], BF16, name="bias_row")
+        nc.vector.memset(bias_row[:], 0.0)
+        bias_all = const.tile([P, H * P], F32, name="bias_all")
+
+        heads = {"A": 4, "B": 4, "C": 4, "E": 1, "F": 3}
+        w_raw, w_grp, w_code, w_scale = {}, {}, {}, {}
+        for k in ("A", "E", "B", "C", "F"):
+            nh = heads[k]
+            w_raw[k] = raw.tile([P, nh * D], BF16, name="w_raw" + k)
+            w_grp[k] = grp.tile([P, nh * D], BF16, name="w_grp" + k, align_bytes=64)
+            w_code[k] = mxp.tile([P, nh * D // 4], U32, name="w_code" + k, align_bytes=64)
+            w_scale[k] = mxp.tile([P, nh * D // 4], U8, name="w_scale" + k, align_bytes=64)
+        x_raw, x_grp, x_code, x_scale = [], [], [], []
+        s_grp, s_code, s_scale = [], [], []
+        o_sb = []
+        for n in range(B):
+            x_raw.append(raw.tile([P, R * D], BF16, name="x_raw%d" % n))
+            x_grp.append(grp.tile([P, R * D], BF16, name="x_grp%d" % n, align_bytes=64))
+            x_code.append(mxp.tile([P, R * D // 4], U32, name="x_code%d" % n, align_bytes=64))
+            x_scale.append(mxp.tile([P, R * D // 4], U8, name="x_scale%d" % n, align_bytes=64))
+            s_grp.append(grp.tile([P, 2 * D], BF16, name="s_grp%d" % n, align_bytes=64))
+            s_code.append(mxp.tile([P, 2 * D // 4], U32, name="s_code%d" % n, align_bytes=64))
+            s_scale.append(mxp.tile([P, 2 * D // 4], U8, name="s_scale%d" % n, align_bytes=64))
+            o_sb.append([outp.tile([P, 4 * R * P], F32, name="o_sb%d_%d" % (n, hf)) for hf in range(2)])
+            nc.vector.memset(s_grp[n][:].bitcast(F32), 0.0)
+
+        nc.scalar.dma_start(out=bias_row[0:1, :], in_=bias.rearrange("(o h) p -> o (h p)", o=1))
+
+        def load_w(k, src, h0, h1):
+            nc.sync.dma_start(
+                out=w_raw[k][:, h0 * D:h1 * D].rearrange("p (h d) -> p h d", h=h1 - h0),
+                in_=src.rearrange("h p d -> p h d"),
+            )
+
+        def load_x(n, r0, r1):
+            nc.sync.dma_start(
+                out=x_raw[n][:, r0 * D:r1 * D],
+                in_=x[n].rearrange("(m r) d -> m (r d)", r=R)[:, r0 * D:r1 * D],
+            )
+
+        load_w("A", w_now[0:2], 0, 2)
+        load_w("A", w_now[2:4], 2, 4)
+        load_x(0, 0, 2)
+        load_x(0, 2, 4)
+        load_w("E", w_back1[0:1], 0, 1)
+        load_x(1, 0, 2)
+        load_x(1, 2, 4)
+        load_w("B", w_now[4:6], 0, 2)
+        load_w("B", w_now[6:8], 2, 4)
+        load_w("C", w_back1[1:3], 0, 2)
+        load_w("C", w_back1[3:5], 2, 4)
+        load_w("F", w_back2[0:3], 0, 3)
+
+        for hf in range(2):
+            bb = apool.tile([P, 512], F32, name="bb", tag="acc")
+            nc.tensor.matmul(bb[:], lhsT=ones[:], rhs=bias_row[:, hf * 512:(hf + 1) * 512], start=True, stop=True)
+            nc.scalar.copy(out=bias_all[:, hf * 512:(hf + 1) * 512], in_=bb[:])
+
+        def copy_on(eng, dst, src):
+            if eng == "v":
+                nc.vector.tensor_copy(out=dst, in_=src)
+            else:
+                nc.scalar.copy(out=dst, in_=src)
+
+        def flip(words):
+            bank = tpool.tile([P, 512], F32, name="bank", tag="bank")
+            for c in range(4):
+                nc.tensor.transpose(bank[:, c * P:(c + 1) * P], words[:, c * P:(c + 1) * P], ident[:])
+            return bank[:].rearrange("q (g u m) -> q g m u", g=G, u=2)
+
+        def quant(src, code, scale, c0, c1):
+            nc.vector.quantize_mx(
+                out=code[:, c0 // 4:c1 // 4].bitcast(FP8X4),
+                scales=scale[:, c0 // 4:c1 // 4],
+                in_=src[:, c0:c1],
+            )
+
+        def prep_w(k, engs):
+            nh = heads[k]
+            dst = w_grp[k][:].bitcast(F32).rearrange("q (g h m u) -> q g h m u", g=G, h=nh, u=2)
+            for h in range(nh):
+                got = flip(w_raw[k][:].bitcast(F32)[:, h * 512:(h + 1) * 512])
+                copy_on(engs[h], dst[:, :, h, :, :], got)
+
+        def quant_w(k):
+            n_cols = heads[k] * D
+            for c0 in range(0, n_cols, 2048):
+                quant(w_grp[k], w_code[k], w_scale[k], c0, min(c0 + 2048, n_cols))
+
+        def prep_x(n, r, eng, eng_s):
+            got = flip(x_raw[n][:].bitcast(F32)[:, r * 512:(r + 1) * 512])
+            dst = x_grp[n][:].bitcast(F32)[:, r * 512:(r + 1) * 512].rearrange("q (g m u) -> q g m u", g=G, u=2)
+            copy_on(eng, dst, got)
+            if r >= 2:
+                i = r - 2
+                dsh = s_grp[n][:].bitcast(F32)[:, i * 512:(i + 1) * 512].rearrange("q (g m u) -> q g m u", g=G, u=2)
+                copy_on(eng_s, dsh[:, :, 1:P, :], got[:, :, 0:P - 1, :])
+
+        def stat(n, r, j, g):
+            rr = r - j
+            if rr >= 0:
+                c = (rr * G + g) * P
+                return x_code[n][:, c:c + P].bitcast(FP8X4), x_scale[n][:, c:c + P]
+            c = ((rr + 2) * G + g) * P
+            return s_code[n][:, c:c + P].bitcast(FP8X4), s_scale[n][:, c:c + P]
+
+        def mx(acc, o0, n, r, j, g, k, c0, width, start, stop):
+            lt, ls = stat(n, r, j, g)
+            nc.tensor.matmul_mx(
+                out=acc[:, o0:o0 + width],
+                lhsT=lt,
+                lhsT_scale=ls,
+                rhs=w_code[k][:, c0:c0 + width].bitcast(FP8X4),
+                rhs_scale=w_scale[k][:, c0:c0 + width],
+                start=start,
+                stop=stop,
+            )
+
+        def leave(acc, n, hf, r):
+            nc.vector.tensor_tensor(
+                out=o_sb[n][hf][:].rearrange("q (h r p) -> q h r p", h=4, r=R)[:, :, r, :],
+                in0=acc[:].rearrange("q (h p) -> q h p", h=4),
+                in1=bias_all[:, hf * 512:(hf + 1) * 512].rearrange("q (h p) -> q h p", h=4),
+                op=ADD,
+            )
+
+        def store(n, hf, r0, r1):
+            nc.sync.dma_start(
+                out=out[n, 4 * hf:4 * hf + 4].rearrange("h (m r) p -> m h r p", r=R)[:, :, r0:r1, :],
+                in_=o_sb[n][hf][:].rearrange("q (h r p) -> q h r p", h=4, r=R)[:, :, r0:r1, :],
+            )
+
+        def low(n):
+            order = (1, 2, 3, 0)
+            accs = {}
+            for r in order:
+                accs[r] = apool.tile([P, 512], F32, name="acc_lo", tag="acc")
+                mx(accs[r], 0, n, r, 0, 0, "A", 0, 512, True, False)
+            for r in order:
+                mx(accs[r], 384, n, r, 1, 0, "E", 0, P, False, False)
+                mx(accs[r], 384, n, r, 1, 1, "E", P, P, False, False)
+                mx(accs[r], 0, n, r, 0, 1, "A", 512, 512, False, True)
+                leave(accs[r], n, 0, r)
+
+        def high(n, r):
+            acc = apool.tile([P, 512], F32, name="acc_hi", tag="acc")
+            for g in range(G):
+                mx(acc, 0, n, r, 0, g, "B", g * 512, 512, g == 0, False)
+                mx(acc, 128, n, r, 2, g, "F", g * 384, 128, False, False)
+                mx(acc, 256, n, r, 2, g, "F", g * 384 + 128, 256, False, False)
+                mx(acc, 0, n, r, 1, g, "C", g * 512, 512, False, g == G - 1)
+            leave(acc, n, 1, r)
+
+        def quant_x(n):
+            quant(x_grp[n], x_code[n], x_scale[n], 0, 2048)
+            quant(x_grp[n], x_code[n], x_scale[n], 2048, 4096)
+            quant(s_grp[n], s_code[n], s_scale[n], 0, 2048)
+
+        prep_w("A", "svsv")
+        prep_x(0, 0, "s", "s")
+        quant_w("A")
+        prep_x(0, 1, "v", "s")
+        prep_x(0, 2, "s", "s")
+        prep_x(0, 3, "v", "s")
+        prep_w("E", "s")
+        quant_x(0)
+        quant_w("E")
+        low(0)
+        store(0, 0, 0, R)
+        prep_x(1, 0, "s", "s")
+        prep_x(1, 1, "v", "s")
+        prep_x(1, 2, "s", "s")
+        prep_x(1, 3, "v", "s")
+        quant_x(1)
+        prep_w("B", "ssss")
+        quant_w("B")
+        low(1)
+        store(1, 0, 0, R)
+        prep_w("C", "ssss")
+        quant_w("C")
+        prep_w("F", "sss")
+        quant_w("F")
+        for r in range(R):
+            high(0, r)
+        store(0, 1, 0, R)
+        for r in range(R):
+            high(1, r)
+            if r % 2 == 1:
+                store(1, 1, r - 1, r + 1)

@@ -24,17 +24,14 @@ def tile_multiheadhomogeneousattention_pa_kernel(tc, x, w_now, w_back1, w_back2,
         grp = ctx.enter_context(tc.tile_pool(name="grp", bufs=1))
         mxp = ctx.enter_context(tc.tile_pool(name="mxp", bufs=1))
         outp = ctx.enter_context(tc.tile_pool(name="outp", bufs=1))
-        tpool = ctx.enter_context(tc.psum_pool(name="tpool", bufs=4))
-        apool = ctx.enter_context(tc.psum_pool(name="apool", bufs=4))
+        psum = ctx.enter_context(tc.psum_pool(name="psum", bufs=8))
+        ctx.enter_context(tc.manual_schedule())
 
         ident = const.tile([P, P], F32, name="ident")
-        make_identity(nc, ident[:])
         ones = const.tile([P, P], BF16, name="ones")
-        nc.vector.memset(ones[:], 1.0)
+        bias_in = const.tile([1, H * P], BF16, name="bias_in")
         bias_row = const.tile([P, H * P], BF16, name="bias_row")
-        nc.vector.memset(bias_row[:], 0.0)
         bias_all = const.tile([P, H * P], F32, name="bias_all")
-
         heads = {"A": 4, "B": 4, "C": 4, "E": 1, "F": 3}
         w_raw, w_grp, w_code, w_scale = {}, {}, {}, {}
         for k in ("A", "E", "B", "C", "F"):
@@ -55,9 +52,6 @@ def tile_multiheadhomogeneousattention_pa_kernel(tc, x, w_now, w_back1, w_back2,
             s_code.append(mxp.tile([P, 2 * D // 4], U32, name="s_code%d" % n, align_bytes=64))
             s_scale.append(mxp.tile([P, 2 * D // 4], U8, name="s_scale%d" % n, align_bytes=64))
             o_sb.append([outp.tile([P, 4 * R * P], F32, name="o_sb%d_%d" % (n, hf)) for hf in range(2)])
-            nc.vector.memset(s_grp[n][:].bitcast(F32), 0.0)
-
-        nc.scalar.dma_start(out=bias_row[0:1, :], in_=bias.rearrange("(o h) p -> o (h p)", o=1))
 
         def load_w(k, src, h0, h1):
             nc.sync.dma_start(
@@ -71,6 +65,7 @@ def tile_multiheadhomogeneousattention_pa_kernel(tc, x, w_now, w_back1, w_back2,
                 in_=x[n].rearrange("(m r) d -> m (r d)", r=R)[:, r0 * D:r1 * D],
             )
 
+        nc.sync.dma_start(out=bias_in[:], in_=bias.rearrange("(o h) p -> o (h p)", o=1))
         load_w("A", w_now[0:2], 0, 2)
         load_w("A", w_now[2:4], 2, 4)
         load_x(0, 0, 2)
@@ -84,10 +79,19 @@ def tile_multiheadhomogeneousattention_pa_kernel(tc, x, w_now, w_back1, w_back2,
         load_w("C", w_back1[3:5], 2, 4)
         load_w("F", w_back2[0:3], 0, 3)
 
+        make_identity(nc, ident[:])
+        nc.vector.memset(ones[:], 1.0)
+        nc.vector.memset(bias_row[:], 0.0)
+        for n in range(B):
+            nc.vector.memset(s_grp[n][:].bitcast(F32), 0.0)
+        nc.vector.tensor_copy(out=bias_row[0:1, :], in_=bias_in[:])
         for hf in range(2):
-            bb = apool.tile([P, 512], F32, name="bb", tag="acc")
+            bb = psum.tile([P, 512], F32, name="bb", tag="bank")
             nc.tensor.matmul(bb[:], lhsT=ones[:], rhs=bias_row[:, hf * 512:(hf + 1) * 512], start=True, stop=True)
             nc.scalar.copy(out=bias_all[:, hf * 512:(hf + 1) * 512], in_=bb[:])
+
+        flipped = {}
+        accs = {}
 
         def copy_on(eng, dst, src):
             if eng == "v":
@@ -96,7 +100,7 @@ def tile_multiheadhomogeneousattention_pa_kernel(tc, x, w_now, w_back1, w_back2,
                 nc.scalar.copy(out=dst, in_=src)
 
         def flip(words):
-            bank = tpool.tile([P, 512], F32, name="bank", tag="bank")
+            bank = psum.tile([P, 512], F32, name="bank", tag="bank")
             for c in range(4):
                 nc.tensor.transpose(bank[:, c * P:(c + 1) * P], words[:, c * P:(c + 1) * P], ident[:])
             return bank[:].rearrange("q (g u m) -> q g m u", g=G, u=2)
@@ -108,26 +112,34 @@ def tile_multiheadhomogeneousattention_pa_kernel(tc, x, w_now, w_back1, w_back2,
                 in_=src[:, c0:c1],
             )
 
-        def prep_w(k, engs):
-            nh = heads[k]
-            dst = w_grp[k][:].bitcast(F32).rearrange("q (g h m u) -> q g h m u", g=G, h=nh, u=2)
-            for h in range(nh):
-                got = flip(w_raw[k][:].bitcast(F32)[:, h * 512:(h + 1) * 512])
-                copy_on(engs[h], dst[:, :, h, :, :], got)
+        def tw(k, h):
+            flipped[(k, h)] = flip(w_raw[k][:].bitcast(F32)[:, h * 512:(h + 1) * 512])
 
-        def quant_w(k):
-            n_cols = heads[k] * D
-            for c0 in range(0, n_cols, 2048):
-                quant(w_grp[k], w_code[k], w_scale[k], c0, min(c0 + 2048, n_cols))
+        def cw(k, h, eng):
+            dst = w_grp[k][:].bitcast(F32).rearrange("q (g h m u) -> q g h m u", g=G, h=heads[k], u=2)
+            copy_on(eng, dst[:, :, h, :, :], flipped[(k, h)])
 
-        def prep_x(n, r, eng, eng_s):
-            got = flip(x_raw[n][:].bitcast(F32)[:, r * 512:(r + 1) * 512])
+        def tx(n, r):
+            flipped[(n, r)] = flip(x_raw[n][:].bitcast(F32)[:, r * 512:(r + 1) * 512])
+
+        def cx(n, r, eng):
             dst = x_grp[n][:].bitcast(F32)[:, r * 512:(r + 1) * 512].rearrange("q (g m u) -> q g m u", g=G, u=2)
-            copy_on(eng, dst, got)
-            if r >= 2:
-                i = r - 2
-                dsh = s_grp[n][:].bitcast(F32)[:, i * 512:(i + 1) * 512].rearrange("q (g m u) -> q g m u", g=G, u=2)
-                copy_on(eng_s, dsh[:, :, 1:P, :], got[:, :, 0:P - 1, :])
+            copy_on(eng, dst, flipped[(n, r)])
+
+        def sh(n, r):
+            nc.vector.tensor_copy(
+                out=s_grp[n][:].rearrange("q (t g c) -> q t g c", t=2, g=G)[:, r - 2, :, 4:512],
+                in_=x_grp[n][:].rearrange("q (t g c) -> q t g c", t=R, g=G)[:, r, :, 0:508],
+            )
+
+        def qw(k, c0, c1):
+            quant(w_grp[k], w_code[k], w_scale[k], c0, c1)
+
+        def qx(n, c0, c1):
+            quant(x_grp[n], x_code[n], x_scale[n], c0, c1)
+
+        def qs(n, c0, c1):
+            quant(s_grp[n], s_code[n], s_scale[n], c0, c1)
 
         def stat(n, r, j, g):
             rr = r - j
@@ -137,10 +149,12 @@ def tile_multiheadhomogeneousattention_pa_kernel(tc, x, w_now, w_back1, w_back2,
             c = ((rr + 2) * G + g) * P
             return s_code[n][:, c:c + P].bitcast(FP8X4), s_scale[n][:, c:c + P]
 
-        def mx(acc, o0, n, r, j, g, k, c0, width, start, stop):
+        def mx(n, hf, r, j, g, k, c0, width, o0, start, stop):
+            if start:
+                accs[(n, hf, r)] = psum.tile([P, 512], F32, name="acc", tag="bank")
             lt, ls = stat(n, r, j, g)
             nc.tensor.matmul_mx(
-                out=acc[:, o0:o0 + width],
+                out=accs[(n, hf, r)][:, o0:o0 + width],
                 lhsT=lt,
                 lhsT_scale=ls,
                 rhs=w_code[k][:, c0:c0 + width].bitcast(FP8X4),
@@ -149,74 +163,203 @@ def tile_multiheadhomogeneousattention_pa_kernel(tc, x, w_now, w_back1, w_back2,
                 stop=stop,
             )
 
-        def leave(acc, n, hf, r):
+        def ev(n, hf, r):
             nc.vector.tensor_tensor(
                 out=o_sb[n][hf][:].rearrange("q (h r p) -> q h r p", h=4, r=R)[:, :, r, :],
-                in0=acc[:].rearrange("q (h p) -> q h p", h=4),
+                in0=accs[(n, hf, r)][:].rearrange("q (h p) -> q h p", h=4),
                 in1=bias_all[:, hf * 512:(hf + 1) * 512].rearrange("q (h p) -> q h p", h=4),
                 op=ADD,
             )
 
-        def store(n, hf, r0, r1):
+        def st(n, hf, r0, r1):
             nc.sync.dma_start(
                 out=out[n, 4 * hf:4 * hf + 4].rearrange("h (m r) p -> m h r p", r=R)[:, :, r0:r1, :],
                 in_=o_sb[n][hf][:].rearrange("q (h r p) -> q h r p", h=4, r=R)[:, :, r0:r1, :],
             )
 
-        def low(n):
-            order = (1, 2, 3, 0)
-            accs = {}
-            for r in order:
-                accs[r] = apool.tile([P, 512], F32, name="acc_lo", tag="acc")
-                mx(accs[r], 0, n, r, 0, 0, "A", 0, 512, True, False)
-            for r in order:
-                mx(accs[r], 384, n, r, 1, 0, "E", 0, P, False, False)
-                mx(accs[r], 384, n, r, 1, 1, "E", P, P, False, False)
-                mx(accs[r], 0, n, r, 0, 1, "A", 512, 512, False, True)
-                leave(accs[r], n, 0, r)
-
-        def high(n, r):
-            acc = apool.tile([P, 512], F32, name="acc_hi", tag="acc")
-            for g in range(G):
-                mx(acc, 0, n, r, 0, g, "B", g * 512, 512, g == 0, False)
-                mx(acc, 128, n, r, 2, g, "F", g * 384, 128, False, False)
-                mx(acc, 256, n, r, 2, g, "F", g * 384 + 128, 256, False, False)
-                mx(acc, 0, n, r, 1, g, "C", g * 512, 512, False, g == G - 1)
-            leave(acc, n, 1, r)
-
-        def quant_x(n):
-            quant(x_grp[n], x_code[n], x_scale[n], 0, 2048)
-            quant(x_grp[n], x_code[n], x_scale[n], 2048, 4096)
-            quant(s_grp[n], s_code[n], s_scale[n], 0, 2048)
-
-        prep_w("A", "svsv")
-        prep_x(0, 0, "s", "s")
-        quant_w("A")
-        prep_x(0, 1, "v", "s")
-        prep_x(0, 2, "s", "s")
-        prep_x(0, 3, "v", "s")
-        prep_w("E", "s")
-        quant_x(0)
-        quant_w("E")
-        low(0)
-        store(0, 0, 0, R)
-        prep_x(1, 0, "s", "s")
-        prep_x(1, 1, "v", "s")
-        prep_x(1, 2, "s", "s")
-        prep_x(1, 3, "v", "s")
-        quant_x(1)
-        prep_w("B", "ssss")
-        quant_w("B")
-        low(1)
-        store(1, 0, 0, R)
-        prep_w("C", "ssss")
-        quant_w("C")
-        prep_w("F", "sss")
-        quant_w("F")
-        for r in range(R):
-            high(0, r)
-        store(0, 1, 0, R)
-        for r in range(R):
-            high(1, r)
-            if r % 2 == 1:
-                store(1, 1, r - 1, r + 1)
+        tw("A", 0)
+        tw("A", 1)
+        tw("A", 2)
+        tw("A", 3)
+        cw("A", 0, "s")
+        cw("A", 1, "v")
+        cw("A", 2, "s")
+        cw("A", 3, "v")
+        tx(0, 0)
+        tx(0, 1)
+        qw("A", 0, 2048)
+        cx(0, 0, "s")
+        cx(0, 1, "v")
+        qw("A", 2048, 4096)
+        tx(0, 2)
+        tx(0, 3)
+        qx(0, 0, 2048)
+        cx(0, 2, "s")
+        cx(0, 3, "v")
+        tw("E", 0)
+        cw("E", 0, "s")
+        tx(1, 0)
+        tx(1, 1)
+        qx(0, 2048, 4096)
+        sh(0, 3)
+        qw("E", 0, 1024)
+        qs(0, 1024, 2048)
+        mx(0, 0, 0, 0, 0, "A", 0, 512, 0, True, False)
+        mx(0, 0, 1, 0, 0, "A", 0, 512, 0, True, False)
+        mx(0, 0, 2, 0, 0, "A", 0, 512, 0, True, False)
+        mx(0, 0, 3, 0, 0, "A", 0, 512, 0, True, False)
+        cx(1, 0, "s")
+        cx(1, 1, "s")
+        tx(1, 2)
+        tx(1, 3)
+        cx(1, 2, "s")
+        cx(1, 3, "s")
+        mx(0, 0, 1, 1, 0, "E", 0, 128, 384, False, False)
+        mx(0, 0, 1, 1, 1, "E", 128, 128, 384, False, False)
+        mx(0, 0, 1, 0, 1, "A", 512, 512, 0, False, True)
+        mx(0, 0, 2, 1, 0, "E", 0, 128, 384, False, False)
+        mx(0, 0, 2, 1, 1, "E", 128, 128, 384, False, False)
+        mx(0, 0, 2, 0, 1, "A", 512, 512, 0, False, True)
+        mx(0, 0, 3, 1, 0, "E", 0, 128, 384, False, False)
+        mx(0, 0, 3, 1, 1, "E", 128, 128, 384, False, False)
+        mx(0, 0, 3, 0, 1, "A", 512, 512, 0, False, True)
+        mx(0, 0, 0, 1, 0, "E", 0, 128, 384, False, False)
+        mx(0, 0, 0, 1, 1, "E", 128, 128, 384, False, False)
+        mx(0, 0, 0, 0, 1, "A", 512, 512, 0, False, True)
+        qx(1, 0, 2048)
+        ev(0, 0, 1)
+        qx(1, 2048, 4096)
+        sh(1, 3)
+        qs(1, 1024, 2048)
+        ev(0, 0, 2)
+        ev(0, 0, 3)
+        ev(0, 0, 0)
+        st(0, 0, 0, 4)
+        tw("B", 0)
+        tw("B", 1)
+        tw("B", 2)
+        tw("B", 3)
+        cw("B", 0, "s")
+        cw("B", 1, "s")
+        cw("B", 2, "s")
+        cw("B", 3, "s")
+        mx(1, 0, 0, 0, 0, "A", 0, 512, 0, True, False)
+        mx(1, 0, 1, 0, 0, "A", 0, 512, 0, True, False)
+        mx(1, 0, 2, 0, 0, "A", 0, 512, 0, True, False)
+        mx(1, 0, 3, 0, 0, "A", 0, 512, 0, True, False)
+        mx(1, 0, 1, 1, 0, "E", 0, 128, 384, False, False)
+        mx(1, 0, 1, 1, 1, "E", 128, 128, 384, False, False)
+        mx(1, 0, 1, 0, 1, "A", 512, 512, 0, False, True)
+        mx(1, 0, 2, 1, 0, "E", 0, 128, 384, False, False)
+        mx(1, 0, 2, 1, 1, "E", 128, 128, 384, False, False)
+        mx(1, 0, 2, 0, 1, "A", 512, 512, 0, False, True)
+        mx(1, 0, 3, 1, 0, "E", 0, 128, 384, False, False)
+        mx(1, 0, 3, 1, 1, "E", 128, 128, 384, False, False)
+        mx(1, 0, 3, 0, 1, "A", 512, 512, 0, False, True)
+        mx(1, 0, 0, 1, 0, "E", 0, 128, 384, False, False)
+        mx(1, 0, 0, 1, 1, "E", 128, 128, 384, False, False)
+        mx(1, 0, 0, 0, 1, "A", 512, 512, 0, False, True)
+        qw("B", 0, 2048)
+        qw("B", 2048, 4096)
+        ev(1, 0, 1)
+        ev(1, 0, 2)
+        ev(1, 0, 3)
+        ev(1, 0, 0)
+        st(1, 0, 0, 4)
+        tw("C", 0)
+        tw("C", 1)
+        tw("C", 2)
+        tw("C", 3)
+        cw("C", 0, "s")
+        cw("C", 1, "s")
+        cw("C", 2, "s")
+        cw("C", 3, "s")
+        tw("F", 0)
+        tw("F", 1)
+        tw("F", 2)
+        cw("F", 0, "s")
+        cw("F", 1, "s")
+        cw("F", 2, "s")
+        sh(0, 2)
+        qs(0, 0, 1024)
+        mx(0, 1, 0, 0, 0, "B", 0, 512, 0, True, False)
+        mx(0, 1, 0, 0, 1, "B", 512, 512, 0, False, False)
+        mx(0, 1, 1, 0, 0, "B", 0, 512, 0, True, False)
+        mx(0, 1, 1, 0, 1, "B", 512, 512, 0, False, False)
+        mx(0, 1, 2, 0, 0, "B", 0, 512, 0, True, False)
+        mx(0, 1, 2, 0, 1, "B", 512, 512, 0, False, False)
+        mx(0, 1, 3, 0, 0, "B", 0, 512, 0, True, False)
+        mx(0, 1, 3, 0, 1, "B", 512, 512, 0, False, False)
+        qw("C", 0, 2048)
+        qw("C", 2048, 4096)
+        mx(0, 1, 0, 1, 0, "C", 0, 512, 0, False, False)
+        mx(0, 1, 1, 1, 0, "C", 0, 512, 0, False, False)
+        mx(0, 1, 2, 1, 0, "C", 0, 512, 0, False, False)
+        mx(0, 1, 3, 1, 0, "C", 0, 512, 0, False, False)
+        qw("F", 0, 2048)
+        qw("F", 2048, 3072)
+        sh(1, 2)
+        qs(1, 0, 1024)
+        mx(0, 1, 0, 2, 0, "F", 0, 128, 128, False, False)
+        mx(0, 1, 0, 2, 0, "F", 128, 256, 256, False, False)
+        mx(0, 1, 0, 2, 1, "F", 384, 128, 128, False, False)
+        mx(0, 1, 0, 2, 1, "F", 512, 256, 256, False, False)
+        mx(0, 1, 0, 1, 1, "C", 512, 512, 0, False, True)
+        ev(0, 1, 0)
+        mx(0, 1, 1, 2, 0, "F", 0, 128, 128, False, False)
+        mx(0, 1, 1, 2, 0, "F", 128, 256, 256, False, False)
+        mx(0, 1, 1, 2, 1, "F", 384, 128, 128, False, False)
+        mx(0, 1, 1, 2, 1, "F", 512, 256, 256, False, False)
+        mx(0, 1, 1, 1, 1, "C", 512, 512, 0, False, True)
+        ev(0, 1, 1)
+        mx(0, 1, 2, 2, 0, "F", 0, 128, 128, False, False)
+        mx(0, 1, 2, 2, 0, "F", 128, 256, 256, False, False)
+        mx(0, 1, 2, 2, 1, "F", 384, 128, 128, False, False)
+        mx(0, 1, 2, 2, 1, "F", 512, 256, 256, False, False)
+        mx(0, 1, 2, 1, 1, "C", 512, 512, 0, False, True)
+        ev(0, 1, 2)
+        mx(0, 1, 3, 2, 0, "F", 0, 128, 128, False, False)
+        mx(0, 1, 3, 2, 0, "F", 128, 256, 256, False, False)
+        mx(0, 1, 3, 2, 1, "F", 384, 128, 128, False, False)
+        mx(0, 1, 3, 2, 1, "F", 512, 256, 256, False, False)
+        mx(0, 1, 3, 1, 1, "C", 512, 512, 0, False, True)
+        ev(0, 1, 3)
+        st(0, 1, 0, 4)
+        mx(1, 1, 0, 0, 0, "B", 0, 512, 0, True, False)
+        mx(1, 1, 0, 2, 0, "F", 0, 128, 128, False, False)
+        mx(1, 1, 0, 2, 0, "F", 128, 256, 256, False, False)
+        mx(1, 1, 0, 1, 0, "C", 0, 512, 0, False, False)
+        mx(1, 1, 0, 0, 1, "B", 512, 512, 0, False, False)
+        mx(1, 1, 0, 2, 1, "F", 384, 128, 128, False, False)
+        mx(1, 1, 0, 2, 1, "F", 512, 256, 256, False, False)
+        mx(1, 1, 0, 1, 1, "C", 512, 512, 0, False, True)
+        ev(1, 1, 0)
+        mx(1, 1, 1, 0, 0, "B", 0, 512, 0, True, False)
+        mx(1, 1, 1, 2, 0, "F", 0, 128, 128, False, False)
+        mx(1, 1, 1, 2, 0, "F", 128, 256, 256, False, False)
+        mx(1, 1, 1, 1, 0, "C", 0, 512, 0, False, False)
+        mx(1, 1, 1, 0, 1, "B", 512, 512, 0, False, False)
+        mx(1, 1, 1, 2, 1, "F", 384, 128, 128, False, False)
+        mx(1, 1, 1, 2, 1, "F", 512, 256, 256, False, False)
+        mx(1, 1, 1, 1, 1, "C", 512, 512, 0, False, True)
+        ev(1, 1, 1)
+        st(1, 1, 0, 2)
+        mx(1, 1, 2, 0, 0, "B", 0, 512, 0, True, False)
+        mx(1, 1, 2, 2, 0, "F", 0, 128, 128, False, False)
+        mx(1, 1, 2, 2, 0, "F", 128, 256, 256, False, False)
+        mx(1, 1, 2, 1, 0, "C", 0, 512, 0, False, False)
+        mx(1, 1, 2, 0, 1, "B", 512, 512, 0, False, False)
+        mx(1, 1, 2, 2, 1, "F", 384, 128, 128, False, False)
+        mx(1, 1, 2, 2, 1, "F", 512, 256, 256, False, False)
+        mx(1, 1, 2, 1, 1, "C", 512, 512, 0, False, True)
+        ev(1, 1, 2)
+        mx(1, 1, 3, 0, 0, "B", 0, 512, 0, True, False)
+        mx(1, 1, 3, 2, 0, "F", 0, 128, 128, False, False)
+        mx(1, 1, 3, 2, 0, "F", 128, 256, 256, False, False)
+        mx(1, 1, 3, 1, 0, "C", 0, 512, 0, False, False)
+        mx(1, 1, 3, 0, 1, "B", 512, 512, 0, False, False)
+        mx(1, 1, 3, 2, 1, "F", 384, 128, 128, False, False)
+        mx(1, 1, 3, 2, 1, "F", 512, 256, 256, False, False)
+        mx(1, 1, 3, 1, 1, "C", 512, 512, 0, False, True)
+        ev(1, 1, 3)
+        st(1, 1, 2, 4)

@@ -163,18 +163,22 @@ def tile_multiheadhomogeneousattention_pa_kernel(tc, x, w_now, w_back1, w_back2,
                 stop=stop,
             )
 
+        span = {0: (0, 0, 4), 1: (1, 0, 4), 2: (1, 0, 2), 3: (1, 2, 2)}
+
         def ev(n, hf, r):
+            hb, h0, nh = span[hf]
             nc.vector.tensor_tensor(
-                out=o_sb[n][hf][:].rearrange("q (h r p) -> q h r p", h=4, r=R)[:, :, r, :],
-                in0=accs[(n, hf, r)][:].rearrange("q (h p) -> q h p", h=4),
-                in1=bias_all[:, hf * 512:(hf + 1) * 512].rearrange("q (h p) -> q h p", h=4),
+                out=o_sb[n][hb][:].rearrange("q (h r p) -> q h r p", h=4, r=R)[:, h0:h0 + nh, r, :],
+                in0=accs[(n, hf, r)][:, h0 * P:(h0 + nh) * P].rearrange("q (h p) -> q h p", h=nh),
+                in1=bias_all[:, (4 * hb + h0) * P:(4 * hb + h0 + nh) * P].rearrange("q (h p) -> q h p", h=nh),
                 op=ADD,
             )
 
         def st(n, hf, r0, r1):
+            hb, h0, nh = span[hf]
             nc.sync.dma_start(
-                out=out[n, 4 * hf:4 * hf + 4].rearrange("h (m r) p -> m h r p", r=R)[:, :, r0:r1, :],
-                in_=o_sb[n][hf][:].rearrange("q (h r p) -> q h r p", h=4, r=R)[:, :, r0:r1, :],
+                out=out[n, 4 * hb + h0:4 * hb + h0 + nh].rearrange("h (m r) p -> m h r p", r=R)[:, :, r0:r1, :],
+                in_=o_sb[n][hb][:].rearrange("q (h r p) -> q h r p", h=4, r=R)[:, h0:h0 + nh, r0:r1, :],
             )
 
         tw("A", 0)
@@ -353,13 +357,20 @@ def tile_multiheadhomogeneousattention_pa_kernel(tc, x, w_now, w_back1, w_back2,
         mx(1, 1, 2, 2, 1, "F", 512, 256, 256, False, False)
         mx(1, 1, 2, 1, 1, "C", 512, 512, 0, False, True)
         ev(1, 1, 2)
-        mx(1, 1, 3, 0, 0, "B", 0, 512, 0, True, False)
-        mx(1, 1, 3, 2, 0, "F", 0, 128, 128, False, False)
-        mx(1, 1, 3, 2, 0, "F", 128, 256, 256, False, False)
-        mx(1, 1, 3, 1, 0, "C", 0, 512, 0, False, False)
-        mx(1, 1, 3, 0, 1, "B", 512, 512, 0, False, False)
-        mx(1, 1, 3, 2, 1, "F", 384, 128, 128, False, False)
-        mx(1, 1, 3, 2, 1, "F", 512, 256, 256, False, False)
-        mx(1, 1, 3, 1, 1, "C", 512, 512, 0, False, True)
-        ev(1, 1, 3)
-        st(1, 1, 2, 4)
+        st(1, 1, 2, 3)
+        mx(1, 2, 3, 0, 0, "B", 0, 256, 0, True, False)
+        mx(1, 2, 3, 2, 0, "F", 0, 128, 128, False, False)
+        mx(1, 2, 3, 1, 0, "C", 0, 256, 0, False, False)
+        mx(1, 2, 3, 0, 1, "B", 512, 256, 0, False, False)
+        mx(1, 2, 3, 2, 1, "F", 384, 128, 128, False, False)
+        mx(1, 2, 3, 1, 1, "C", 512, 256, 0, False, True)
+        ev(1, 2, 3)
+        st(1, 2, 3, 4)
+        mx(1, 3, 3, 0, 0, "B", 256, 256, 256, True, False)
+        mx(1, 3, 3, 2, 0, "F", 128, 256, 256, False, False)
+        mx(1, 3, 3, 1, 0, "C", 256, 256, 256, False, False)
+        mx(1, 3, 3, 0, 1, "B", 768, 256, 256, False, False)
+        mx(1, 3, 3, 2, 1, "F", 512, 256, 256, False, False)
+        mx(1, 3, 3, 1, 1, "C", 768, 256, 256, False, True)
+        ev(1, 3, 3)
+        st(1, 3, 3, 4)

@@ -68,8 +68,10 @@ def tile_multiheadhomogeneousattention_pa_kernel(tc, x, w_now, w_back1, w_back2,
         nc.sync.dma_start(out=bias_in[:], in_=bias.rearrange("(o h) p -> o (h p)", o=1))
         load_w("A", w_now[0:2], 0, 2)
         load_w("A", w_now[2:4], 2, 4)
-        load_x(0, 0, 2)
-        load_x(0, 2, 4)
+        load_x(0, 0, 1)
+        load_x(0, 1, 2)
+        load_x(0, 2, 3)
+        load_x(0, 3, 4)
         load_w("E", w_back1[0:1], 0, 1)
         load_x(1, 0, 2)
         load_x(1, 2, 4)
@@ -190,79 +192,80 @@ def tile_multiheadhomogeneousattention_pa_kernel(tc, x, w_now, w_back1, w_back2,
         cw("A", 2, "s")
         cw("A", 3, "v")
         tx(0, 0)
-        tx(0, 1)
-        qw("A", 0, 2048)
         cx(0, 0, "s")
-        cx(0, 1, "v")
+        qw("A", 0, 2048)
+        tx(0, 1)
+        cx(0, 1, "s")
+        qx(0, 0, 1024)
         qw("A", 2048, 4096)
         tx(0, 2)
-        tx(0, 3)
-        qx(0, 0, 2048)
         cx(0, 2, "s")
-        cx(0, 3, "v")
+        qx(0, 1024, 2048)
+        tx(0, 3)
+        cx(0, 3, "s")
+        mx(0, 0, 0, 0, 0, "A", 0, 512, 0, True, False)
+        mx(0, 0, 0, 0, 1, "A", 512, 512, 0, False, False)
+        mx(0, 0, 1, 0, 0, "A", 0, 512, 0, True, False)
+        mx(0, 0, 1, 0, 1, "A", 512, 512, 0, False, False)
         tw("E", 0)
         cw("E", 0, "s")
-        tx(1, 0)
-        tx(1, 1)
         qx(0, 2048, 4096)
         sh(0, 3)
-        qw("E", 0, 1024)
-        qs(0, 1024, 2048)
-        mx(0, 0, 0, 0, 0, "A", 0, 512, 0, True, False)
-        mx(0, 0, 1, 0, 0, "A", 0, 512, 0, True, False)
-        mx(0, 0, 2, 0, 0, "A", 0, 512, 0, True, False)
-        mx(0, 0, 3, 0, 0, "A", 0, 512, 0, True, False)
+        tx(1, 0)
+        tx(1, 1)
         cx(1, 0, "s")
         cx(1, 1, "s")
+        mx(0, 0, 2, 0, 0, "A", 0, 512, 0, True, False)
+        mx(0, 0, 2, 0, 1, "A", 512, 512, 0, False, False)
+        mx(0, 0, 3, 0, 0, "A", 0, 512, 0, True, False)
+        mx(0, 0, 3, 0, 1, "A", 512, 512, 0, False, False)
+        qw("E", 0, 1024)
+        qs(0, 1024, 2048)
+        mx(0, 0, 1, 1, 0, "E", 0, 128, 384, False, False)
+        mx(0, 0, 1, 1, 1, "E", 128, 128, 384, False, True)
+        mx(0, 0, 2, 1, 0, "E", 0, 128, 384, False, False)
+        mx(0, 0, 2, 1, 1, "E", 128, 128, 384, False, True)
+        mx(0, 0, 3, 1, 0, "E", 0, 128, 384, False, False)
+        mx(0, 0, 3, 1, 1, "E", 128, 128, 384, False, True)
+        mx(0, 0, 0, 1, 0, "E", 0, 128, 384, False, False)
+        mx(0, 0, 0, 1, 1, "E", 128, 128, 384, False, True)
         tx(1, 2)
         tx(1, 3)
         cx(1, 2, "s")
         cx(1, 3, "s")
-        mx(0, 0, 1, 1, 0, "E", 0, 128, 384, False, False)
-        mx(0, 0, 1, 1, 1, "E", 128, 128, 384, False, False)
-        mx(0, 0, 1, 0, 1, "A", 512, 512, 0, False, True)
-        mx(0, 0, 2, 1, 0, "E", 0, 128, 384, False, False)
-        mx(0, 0, 2, 1, 1, "E", 128, 128, 384, False, False)
-        mx(0, 0, 2, 0, 1, "A", 512, 512, 0, False, True)
-        mx(0, 0, 3, 1, 0, "E", 0, 128, 384, False, False)
-        mx(0, 0, 3, 1, 1, "E", 128, 128, 384, False, False)
-        mx(0, 0, 3, 0, 1, "A", 512, 512, 0, False, True)
-        mx(0, 0, 0, 1, 0, "E", 0, 128, 384, False, False)
-        mx(0, 0, 0, 1, 1, "E", 128, 128, 384, False, False)
-        mx(0, 0, 0, 0, 1, "A", 512, 512, 0, False, True)
-        qx(1, 0, 2048)
-        ev(0, 0, 1)
-        qx(1, 2048, 4096)
-        sh(1, 3)
-        qs(1, 1024, 2048)
-        ev(0, 0, 2)
-        ev(0, 0, 3)
-        ev(0, 0, 0)
-        st(0, 0, 0, 4)
         tw("B", 0)
         tw("B", 1)
         tw("B", 2)
         tw("B", 3)
+        qx(1, 0, 2048)
+        ev(0, 0, 1)
+        ev(0, 0, 2)
+        qx(1, 2048, 4096)
+        sh(1, 3)
+        qs(1, 1024, 2048)
+        ev(0, 0, 3)
+        ev(0, 0, 0)
+        st(0, 0, 0, 4)
         cw("B", 0, "s")
         cw("B", 1, "s")
         cw("B", 2, "s")
         cw("B", 3, "s")
         mx(1, 0, 0, 0, 0, "A", 0, 512, 0, True, False)
+        mx(1, 0, 0, 0, 1, "A", 512, 512, 0, False, False)
         mx(1, 0, 1, 0, 0, "A", 0, 512, 0, True, False)
+        mx(1, 0, 1, 0, 1, "A", 512, 512, 0, False, False)
         mx(1, 0, 2, 0, 0, "A", 0, 512, 0, True, False)
+        mx(1, 0, 2, 0, 1, "A", 512, 512, 0, False, False)
         mx(1, 0, 3, 0, 0, "A", 0, 512, 0, True, False)
+        mx(1, 0, 3, 0, 1, "A", 512, 512, 0, False, False)
         mx(1, 0, 1, 1, 0, "E", 0, 128, 384, False, False)
-        mx(1, 0, 1, 1, 1, "E", 128, 128, 384, False, False)
-        mx(1, 0, 1, 0, 1, "A", 512, 512, 0, False, True)
+        mx(1, 0, 1, 1, 1, "E", 128, 128, 384, False, True)
         mx(1, 0, 2, 1, 0, "E", 0, 128, 384, False, False)
-        mx(1, 0, 2, 1, 1, "E", 128, 128, 384, False, False)
-        mx(1, 0, 2, 0, 1, "A", 512, 512, 0, False, True)
+        mx(1, 0, 2, 1, 1, "E", 128, 128, 384, False, True)
         mx(1, 0, 3, 1, 0, "E", 0, 128, 384, False, False)
-        mx(1, 0, 3, 1, 1, "E", 128, 128, 384, False, False)
-        mx(1, 0, 3, 0, 1, "A", 512, 512, 0, False, True)
+        mx(1, 0, 3, 1, 1, "E", 128, 128, 384, False, True)
         mx(1, 0, 0, 1, 0, "E", 0, 128, 384, False, False)
-        mx(1, 0, 0, 1, 1, "E", 128, 128, 384, False, False)
-        mx(1, 0, 0, 0, 1, "A", 512, 512, 0, False, True)
+        mx(1, 0, 0, 1, 1, "E", 128, 128, 384, False, True)
         qw("B", 0, 2048)
         qw("B", 2048, 4096)
         ev(1, 0, 1)

@@ -8,372 +8,245 @@ BF16 = mybir.dt.bfloat16
 U32 = mybir.dt.uint32
 U8 = mybir.dt.uint8
 FP8X4 = mybir.dt.float8_e4m3fn_x4
-ADD = mybir.AluOpType.add
 
 B, S, D, P, H = 2, 512, 1024, 128, 8
-R = 4
-G = 2
-FLOPS = 2 * B * S * D * P * 16
+R = S // P
+G = D // (4 * P)
+BANK = 512
+FLOPS = 2 * B * S * D * P * (8 + 5 + 3)
+
+WEIGHT_TILES = {"now_lo": 4, "back1_lo": 1, "now_hi": 4, "back1_hi": 4, "back2": 3}
+
+BANKS = {
+    "low": (0, 4, {0: [("now_lo", 0, 4, 0)], 1: [("back1_lo", 0, 1, 3)]}),
+    "high": (4, 4, {0: [("now_hi", 0, 4, 4)], 1: [("back1_hi", 0, 4, 4)], 2: [("back2", 0, 1, 5), ("back2", 1, 2, 6)]}),
+    "high_left": (4, 2, {0: [("now_hi", 0, 2, 4)], 1: [("back1_hi", 0, 2, 4)], 2: [("back2", 0, 1, 5)]}),
+    "high_right": (6, 2, {0: [("now_hi", 2, 2, 6)], 1: [("back1_hi", 2, 2, 6)], 2: [("back2", 1, 2, 6)]}),
+}
+HIGH_AT_ONCE = [(0, 0), (2, 0), (1, 0), (0, 1), (2, 1), (1, 1)]
 
 
 def tile_multiheadhomogeneousattention_pa_kernel(tc, x, w_now, w_back1, w_back2, bias, out):
     nc = tc.nc
     with ExitStack() as ctx:
         const = ctx.enter_context(tc.tile_pool(name="const", bufs=1))
-        raw = ctx.enter_context(tc.tile_pool(name="raw", bufs=1))
-        grp = ctx.enter_context(tc.tile_pool(name="grp", bufs=1))
-        mxp = ctx.enter_context(tc.tile_pool(name="mxp", bufs=1))
-        outp = ctx.enter_context(tc.tile_pool(name="outp", bufs=1))
+        raw_pool = ctx.enter_context(tc.tile_pool(name="raw", bufs=1))
+        grouped_pool = ctx.enter_context(tc.tile_pool(name="grouped", bufs=1))
+        mx_pool = ctx.enter_context(tc.tile_pool(name="mx", bufs=1))
+        out_pool = ctx.enter_context(tc.tile_pool(name="outp", bufs=1))
         psum = ctx.enter_context(tc.psum_pool(name="psum", bufs=8))
         ctx.enter_context(tc.manual_schedule())
 
-        ident = const.tile([P, P], F32, name="ident")
+        tiles_of = dict(WEIGHT_TILES)
+        moved = ["moved%d" % n for n in range(B)]
+        for n in range(B):
+            tiles_of["x%d" % n] = R
+            tiles_of[moved[n]] = 2
+        raw, grouped, words, scales = {}, {}, {}, {}
+        for name in sorted(tiles_of):
+            cols = tiles_of[name] * D
+            if name not in moved:
+                raw[name] = raw_pool.tile([P, cols], BF16, name="raw_" + name)
+            grouped[name] = grouped_pool.tile([P, cols], BF16, name="grouped_" + name, align_bytes=64)
+            words[name] = mx_pool.tile([P, cols // 4], U32, name="words_" + name, align_bytes=64)
+            scales[name] = mx_pool.tile([P, cols // 4], U8, name="scales_" + name, align_bytes=64)
+        y_sb = {}
+        for n in range(B):
+            for half in range(2):
+                y_sb[(n, half)] = out_pool.tile([P, 4 * R * P], F32, name="y_sb%d%d" % (n, half))
+        identity = const.tile([P, P], F32, name="identity")
         ones = const.tile([P, P], BF16, name="ones")
         bias_in = const.tile([1, H * P], BF16, name="bias_in")
         bias_row = const.tile([P, H * P], BF16, name="bias_row")
         bias_all = const.tile([P, H * P], F32, name="bias_all")
-        heads = {"A": 4, "B": 4, "C": 4, "E": 1, "F": 3}
-        w_raw, w_grp, w_code, w_scale = {}, {}, {}, {}
-        for k in ("A", "E", "B", "C", "F"):
-            nh = heads[k]
-            w_raw[k] = raw.tile([P, nh * D], BF16, name="w_raw" + k)
-            w_grp[k] = grp.tile([P, nh * D], BF16, name="w_grp" + k, align_bytes=64)
-            w_code[k] = mxp.tile([P, nh * D // 4], U32, name="w_code" + k, align_bytes=64)
-            w_scale[k] = mxp.tile([P, nh * D // 4], U8, name="w_scale" + k, align_bytes=64)
-        x_raw, x_grp, x_code, x_scale = [], [], [], []
-        s_grp, s_code, s_scale = [], [], []
-        o_sb = []
-        for n in range(B):
-            x_raw.append(raw.tile([P, R * D], BF16, name="x_raw%d" % n))
-            x_grp.append(grp.tile([P, R * D], BF16, name="x_grp%d" % n, align_bytes=64))
-            x_code.append(mxp.tile([P, R * D // 4], U32, name="x_code%d" % n, align_bytes=64))
-            x_scale.append(mxp.tile([P, R * D // 4], U8, name="x_scale%d" % n, align_bytes=64))
-            s_grp.append(grp.tile([P, 2 * D], BF16, name="s_grp%d" % n, align_bytes=64))
-            s_code.append(mxp.tile([P, 2 * D // 4], U32, name="s_code%d" % n, align_bytes=64))
-            s_scale.append(mxp.tile([P, 2 * D // 4], U8, name="s_scale%d" % n, align_bytes=64))
-            o_sb.append([outp.tile([P, 4 * R * P], F32, name="o_sb%d_%d" % (n, hf)) for hf in range(2)])
 
-        def load_w(k, src, h0, h1):
+        def load_w(name, src, t0, t1):
             nc.sync.dma_start(
-                out=w_raw[k][:, h0 * D:h1 * D].rearrange("p (h d) -> p h d", h=h1 - h0),
-                in_=src.rearrange("h p d -> p h d"),
+                out=raw[name][:, t0 * D:t1 * D].rearrange("p (t d) -> p t d", t=t1 - t0),
+                in_=src[t0:t1].rearrange("t p d -> p t d"),
             )
 
         def load_x(n, r0, r1):
             nc.sync.dma_start(
-                out=x_raw[n][:, r0 * D:r1 * D],
+                out=raw["x%d" % n][:, r0 * D:r1 * D],
                 in_=x[n].rearrange("(m r) d -> m (r d)", r=R)[:, r0 * D:r1 * D],
             )
 
         nc.sync.dma_start(out=bias_in[:], in_=bias.rearrange("(o h) p -> o (h p)", o=1))
-        load_w("A", w_now[0:2], 0, 2)
-        load_w("A", w_now[2:4], 2, 4)
-        load_x(0, 0, 1)
-        load_x(0, 1, 2)
-        load_x(0, 2, 3)
-        load_x(0, 3, 4)
-        load_w("E", w_back1[0:1], 0, 1)
+        load_w("now_lo", w_now[0:4], 0, 2)
+        load_w("now_lo", w_now[0:4], 2, 4)
+        load_x(0, 0, 2)
+        load_x(0, 2, 4)
+        load_w("back1_lo", w_back1[0:1], 0, 1)
         load_x(1, 0, 2)
         load_x(1, 2, 4)
-        load_w("B", w_now[4:6], 0, 2)
-        load_w("B", w_now[6:8], 2, 4)
-        load_w("C", w_back1[1:3], 0, 2)
-        load_w("C", w_back1[3:5], 2, 4)
-        load_w("F", w_back2[0:3], 0, 3)
+        load_w("now_hi", w_now[4:8], 0, 2)
+        load_w("now_hi", w_now[4:8], 2, 4)
+        load_w("back1_hi", w_back1[1:5], 0, 2)
+        load_w("back1_hi", w_back1[1:5], 2, 4)
+        load_w("back2", w_back2, 0, 3)
 
-        make_identity(nc, ident[:])
+        make_identity(nc, identity[:])
         nc.vector.memset(ones[:], 1.0)
         nc.vector.memset(bias_row[:], 0.0)
         for n in range(B):
-            nc.vector.memset(s_grp[n][:].bitcast(F32), 0.0)
+            nc.vector.memset(grouped["moved%d" % n][:].bitcast(F32), 0.0)
         nc.vector.tensor_copy(out=bias_row[0:1, :], in_=bias_in[:])
-        for hf in range(2):
-            bb = psum.tile([P, 512], F32, name="bb", tag="bank")
-            nc.tensor.matmul(bb[:], lhsT=ones[:], rhs=bias_row[:, hf * 512:(hf + 1) * 512], start=True, stop=True)
-            nc.scalar.copy(out=bias_all[:, hf * 512:(hf + 1) * 512], in_=bb[:])
+        for half in range(2):
+            spread = psum.tile([P, BANK], F32, name="spread", tag="bank")
+            cols = slice(half * BANK, (half + 1) * BANK)
+            nc.tensor.matmul(spread[:], lhsT=ones[:], rhs=bias_row[:, cols], start=True, stop=True)
+            nc.scalar.copy(out=bias_all[:, cols], in_=spread[:])
 
         flipped = {}
-        accs = {}
+        acc = {}
 
-        def copy_on(eng, dst, src):
-            if eng == "v":
-                nc.vector.tensor_copy(out=dst, in_=src)
-            else:
-                nc.scalar.copy(out=dst, in_=src)
+        def word_column(name, t, g):
+            if name in WEIGHT_TILES:
+                return (g * tiles_of[name] + t) * P
+            return (t * G + g) * P
 
-        def flip(words):
-            bank = psum.tile([P, 512], F32, name="bank", tag="bank")
-            for c in range(4):
-                nc.tensor.transpose(bank[:, c * P:(c + 1) * P], words[:, c * P:(c + 1) * P], ident[:])
-            return bank[:].rearrange("q (g u m) -> q g m u", g=G, u=2)
+        def flip(name, tiles):
+            for t in tiles:
+                bank = psum.tile([P, BANK], F32, name="bank", tag="bank")
+                for c in range(4):
+                    first = t * BANK + c * P
+                    nc.tensor.transpose(bank[:, c * P:(c + 1) * P], raw[name][:].bitcast(F32)[:, first:first + P], identity[:])
+                flipped[(name, t)] = bank
 
-        def quant(src, code, scale, c0, c1):
-            nc.vector.quantize_mx(
-                out=code[:, c0 // 4:c1 // 4].bitcast(FP8X4),
-                scales=scale[:, c0 // 4:c1 // 4],
-                in_=src[:, c0:c1],
-            )
+        def copy_out(name, tiles, engines):
+            order = "q (g t m u) -> q g t m u" if name in WEIGHT_TILES else "q (t g m u) -> q g t m u"
+            dst = grouped[name][:].bitcast(F32).rearrange(order, g=G, t=tiles_of[name], u=2)
+            for t, engine in zip(tiles, engines):
+                src = flipped[(name, t)][:].rearrange("q (g u m) -> q g m u", g=G, u=2)
+                if engine == "vector":
+                    nc.vector.tensor_copy(out=dst[:, :, t, :, :], in_=src)
+                else:
+                    nc.scalar.copy(out=dst[:, :, t, :, :], in_=src)
 
-        def tw(k, h):
-            flipped[(k, h)] = flip(w_raw[k][:].bitcast(F32)[:, h * 512:(h + 1) * 512])
-
-        def cw(k, h, eng):
-            dst = w_grp[k][:].bitcast(F32).rearrange("q (g h m u) -> q g h m u", g=G, h=heads[k], u=2)
-            copy_on(eng, dst[:, :, h, :, :], flipped[(k, h)])
-
-        def tx(n, r):
-            flipped[(n, r)] = flip(x_raw[n][:].bitcast(F32)[:, r * 512:(r + 1) * 512])
-
-        def cx(n, r, eng):
-            dst = x_grp[n][:].bitcast(F32)[:, r * 512:(r + 1) * 512].rearrange("q (g m u) -> q g m u", g=G, u=2)
-            copy_on(eng, dst, flipped[(n, r)])
-
-        def sh(n, r):
+        def move(n, r):
             nc.vector.tensor_copy(
-                out=s_grp[n][:].rearrange("q (t g c) -> q t g c", t=2, g=G)[:, r - 2, :, 4:512],
-                in_=x_grp[n][:].rearrange("q (t g c) -> q t g c", t=R, g=G)[:, r, :, 0:508],
+                out=grouped["moved%d" % n][:].rearrange("q (t g c) -> q t g c", t=2, g=G)[:, r - 2, :, 4:4 * P],
+                in_=grouped["x%d" % n][:].rearrange("q (t g c) -> q t g c", t=R, g=G)[:, r, :, 0:4 * P - 4],
             )
 
-        def qw(k, c0, c1):
-            quant(w_grp[k], w_code[k], w_scale[k], c0, c1)
-
-        def qx(n, c0, c1):
-            quant(x_grp[n], x_code[n], x_scale[n], c0, c1)
-
-        def qs(n, c0, c1):
-            quant(s_grp[n], s_code[n], s_scale[n], c0, c1)
-
-        def stat(n, r, j, g):
-            rr = r - j
-            if rr >= 0:
-                c = (rr * G + g) * P
-                return x_code[n][:, c:c + P].bitcast(FP8X4), x_scale[n][:, c:c + P]
-            c = ((rr + 2) * G + g) * P
-            return s_code[n][:, c:c + P].bitcast(FP8X4), s_scale[n][:, c:c + P]
-
-        def mx(n, hf, r, j, g, k, c0, width, o0, start, stop):
-            if start:
-                accs[(n, hf, r)] = psum.tile([P, 512], F32, name="acc", tag="bank")
-            lt, ls = stat(n, r, j, g)
-            nc.tensor.matmul_mx(
-                out=accs[(n, hf, r)][:, o0:o0 + width],
-                lhsT=lt,
-                lhsT_scale=ls,
-                rhs=w_code[k][:, c0:c0 + width].bitcast(FP8X4),
-                rhs_scale=w_scale[k][:, c0:c0 + width],
-                start=start,
-                stop=stop,
+        def quantise(name, c0, c1):
+            nc.vector.quantize_mx(
+                out=words[name][:, c0 // 4:c1 // 4].bitcast(FP8X4),
+                scales=scales[name][:, c0 // 4:c1 // 4],
+                in_=grouped[name][:, c0:c1],
             )
 
-        span = {0: (0, 0, 4), 1: (1, 0, 4), 2: (1, 0, 2), 3: (1, 2, 2)}
+        def passes(n, kind, r, todo, begin=False, end=False):
+            if begin:
+                acc[(n, kind, r)] = psum.tile([P, BANK], F32, name="acc", tag="bank")
+            pieces = [(tap, g, piece) for tap, g in todo for piece in BANKS[kind][2][tap]]
+            for i, (tap, g, (name, t0, count, head)) in enumerate(pieces):
+                tokens, t = ("x%d" % n, r - tap) if r >= tap else ("moved%d" % n, r - tap + 2)
+                a = word_column(tokens, t, g)
+                b = word_column(name, t0, g)
+                o = (head % 4) * P
+                nc.tensor.matmul_mx(
+                    out=acc[(n, kind, r)][:, o:o + count * P],
+                    lhsT=words[tokens][:, a:a + P].bitcast(FP8X4),
+                    lhsT_scale=scales[tokens][:, a:a + P],
+                    rhs=words[name][:, b:b + count * P].bitcast(FP8X4),
+                    rhs_scale=scales[name][:, b:b + count * P],
+                    start=begin and i == 0,
+                    stop=end and i == len(pieces) - 1,
+                )
 
-        def ev(n, hf, r):
-            hb, h0, nh = span[hf]
+        def leave(n, kind, r):
+            head, count = BANKS[kind][0], BANKS[kind][1]
+            h0 = head % 4
             nc.vector.tensor_tensor(
-                out=o_sb[n][hb][:].rearrange("q (h r p) -> q h r p", h=4, r=R)[:, h0:h0 + nh, r, :],
-                in0=accs[(n, hf, r)][:, h0 * P:(h0 + nh) * P].rearrange("q (h p) -> q h p", h=nh),
-                in1=bias_all[:, (4 * hb + h0) * P:(4 * hb + h0 + nh) * P].rearrange("q (h p) -> q h p", h=nh),
-                op=ADD,
+                out=y_sb[(n, head // 4)][:].rearrange("q (h r p) -> q h r p", h=4, r=R)[:, h0:h0 + count, r, :],
+                in0=acc[(n, kind, r)][:, h0 * P:(h0 + count) * P].rearrange("q (h p) -> q h p", h=count),
+                in1=bias_all[:, head * P:(head + count) * P].rearrange("q (h p) -> q h p", h=count),
+                op=mybir.AluOpType.add,
             )
 
-        def st(n, hf, r0, r1):
-            hb, h0, nh = span[hf]
+        def store(n, kind, r0, r1):
+            head, count = BANKS[kind][0], BANKS[kind][1]
+            h0 = head % 4
             nc.sync.dma_start(
-                out=out[n, 4 * hb + h0:4 * hb + h0 + nh].rearrange("h (m r) p -> m h r p", r=R)[:, :, r0:r1, :],
-                in_=o_sb[n][hb][:].rearrange("q (h r p) -> q h r p", h=4, r=R)[:, h0:h0 + nh, r0:r1, :],
+                out=out[n, head:head + count].rearrange("h (m r) p -> m h r p", r=R)[:, :, r0:r1, :],
+                in_=y_sb[(n, head // 4)][:].rearrange("q (h r p) -> q h r p", h=4, r=R)[:, h0:h0 + count, r0:r1, :],
             )
 
-        tw("A", 0)
-        tw("A", 1)
-        tw("A", 2)
-        tw("A", 3)
-        cw("A", 0, "s")
-        cw("A", 1, "v")
-        cw("A", 2, "s")
-        cw("A", 3, "v")
-        tx(0, 0)
-        cx(0, 0, "s")
-        qw("A", 0, 2048)
-        tx(0, 1)
-        cx(0, 1, "s")
-        qx(0, 0, 1024)
-        qw("A", 2048, 4096)
-        tx(0, 2)
-        cx(0, 2, "s")
-        qx(0, 1024, 2048)
-        tx(0, 3)
-        cx(0, 3, "s")
-        mx(0, 0, 0, 0, 0, "A", 0, 512, 0, True, False)
-        mx(0, 0, 0, 0, 1, "A", 512, 512, 0, False, False)
-        mx(0, 0, 1, 0, 0, "A", 0, 512, 0, True, False)
-        mx(0, 0, 1, 0, 1, "A", 512, 512, 0, False, False)
-        tw("E", 0)
-        cw("E", 0, "s")
-        qx(0, 2048, 4096)
-        sh(0, 3)
-        tx(1, 0)
-        tx(1, 1)
-        cx(1, 0, "s")
-        cx(1, 1, "s")
-        mx(0, 0, 2, 0, 0, "A", 0, 512, 0, True, False)
-        mx(0, 0, 2, 0, 1, "A", 512, 512, 0, False, False)
-        mx(0, 0, 3, 0, 0, "A", 0, 512, 0, True, False)
-        mx(0, 0, 3, 0, 1, "A", 512, 512, 0, False, False)
-        qw("E", 0, 1024)
-        qs(0, 1024, 2048)
-        mx(0, 0, 1, 1, 0, "E", 0, 128, 384, False, False)
-        mx(0, 0, 1, 1, 1, "E", 128, 128, 384, False, True)
-        mx(0, 0, 2, 1, 0, "E", 0, 128, 384, False, False)
-        mx(0, 0, 2, 1, 1, "E", 128, 128, 384, False, True)
-        mx(0, 0, 3, 1, 0, "E", 0, 128, 384, False, False)
-        mx(0, 0, 3, 1, 1, "E", 128, 128, 384, False, True)
-        mx(0, 0, 0, 1, 0, "E", 0, 128, 384, False, False)
-        mx(0, 0, 0, 1, 1, "E", 128, 128, 384, False, True)
-        tx(1, 2)
-        tx(1, 3)
-        cx(1, 2, "s")
-        cx(1, 3, "s")
-        tw("B", 0)
-        tw("B", 1)
-        tw("B", 2)
-        tw("B", 3)
-        qx(1, 0, 2048)
-        ev(0, 0, 1)
-        ev(0, 0, 2)
-        qx(1, 2048, 4096)
-        sh(1, 3)
-        qs(1, 1024, 2048)
-        ev(0, 0, 3)
-        ev(0, 0, 0)
-        st(0, 0, 0, 4)
-        cw("B", 0, "s")
-        cw("B", 1, "s")
-        cw("B", 2, "s")
-        cw("B", 3, "s")
-        mx(1, 0, 0, 0, 0, "A", 0, 512, 0, True, False)
-        mx(1, 0, 0, 0, 1, "A", 512, 512, 0, False, False)
-        mx(1, 0, 1, 0, 0, "A", 0, 512, 0, True, False)
-        mx(1, 0, 1, 0, 1, "A", 512, 512, 0, False, False)
-        mx(1, 0, 2, 0, 0, "A", 0, 512, 0, True, False)
-        mx(1, 0, 2, 0, 1, "A", 512, 512, 0, False, False)
-        mx(1, 0, 3, 0, 0, "A", 0, 512, 0, True, False)
-        mx(1, 0, 3, 0, 1, "A", 512, 512, 0, False, False)
-        mx(1, 0, 1, 1, 0, "E", 0, 128, 384, False, False)
-        mx(1, 0, 1, 1, 1, "E", 128, 128, 384, False, True)
-        mx(1, 0, 2, 1, 0, "E", 0, 128, 384, False, False)
-        mx(1, 0, 2, 1, 1, "E", 128, 128, 384, False, True)
-        mx(1, 0, 3, 1, 0, "E", 0, 128, 384, False, False)
-        mx(1, 0, 3, 1, 1, "E", 128, 128, 384, False, True)
-        mx(1, 0, 0, 1, 0, "E", 0, 128, 384, False, False)
-        mx(1, 0, 0, 1, 1, "E", 128, 128, 384, False, True)
-        qw("B", 0, 2048)
-        qw("B", 2048, 4096)
-        ev(1, 0, 1)
-        ev(1, 0, 2)
-        ev(1, 0, 3)
-        ev(1, 0, 0)
-        st(1, 0, 0, 4)
-        tw("C", 0)
-        tw("C", 1)
-        tw("C", 2)
-        tw("C", 3)
-        cw("C", 0, "s")
-        cw("C", 1, "s")
-        cw("C", 2, "s")
-        cw("C", 3, "s")
-        tw("F", 0)
-        tw("F", 1)
-        tw("F", 2)
-        cw("F", 0, "s")
-        cw("F", 1, "s")
-        cw("F", 2, "s")
-        sh(0, 2)
-        qs(0, 0, 1024)
-        mx(0, 1, 0, 0, 0, "B", 0, 512, 0, True, False)
-        mx(0, 1, 0, 0, 1, "B", 512, 512, 0, False, False)
-        mx(0, 1, 1, 0, 0, "B", 0, 512, 0, True, False)
-        mx(0, 1, 1, 0, 1, "B", 512, 512, 0, False, False)
-        mx(0, 1, 2, 0, 0, "B", 0, 512, 0, True, False)
-        mx(0, 1, 2, 0, 1, "B", 512, 512, 0, False, False)
-        mx(0, 1, 3, 0, 0, "B", 0, 512, 0, True, False)
-        mx(0, 1, 3, 0, 1, "B", 512, 512, 0, False, False)
-        qw("C", 0, 2048)
-        qw("C", 2048, 4096)
-        mx(0, 1, 0, 1, 0, "C", 0, 512, 0, False, False)
-        mx(0, 1, 1, 1, 0, "C", 0, 512, 0, False, False)
-        mx(0, 1, 2, 1, 0, "C", 0, 512, 0, False, False)
-        mx(0, 1, 3, 1, 0, "C", 0, 512, 0, False, False)
-        qw("F", 0, 2048)
-        qw("F", 2048, 3072)
-        sh(1, 2)
-        qs(1, 0, 1024)
-        mx(0, 1, 0, 2, 0, "F", 0, 128, 128, False, False)
-        mx(0, 1, 0, 2, 0, "F", 128, 256, 256, False, False)
-        mx(0, 1, 0, 2, 1, "F", 384, 128, 128, False, False)
-        mx(0, 1, 0, 2, 1, "F", 512, 256, 256, False, False)
-        mx(0, 1, 0, 1, 1, "C", 512, 512, 0, False, True)
-        ev(0, 1, 0)
-        mx(0, 1, 1, 2, 0, "F", 0, 128, 128, False, False)
-        mx(0, 1, 1, 2, 0, "F", 128, 256, 256, False, False)
-        mx(0, 1, 1, 2, 1, "F", 384, 128, 128, False, False)
-        mx(0, 1, 1, 2, 1, "F", 512, 256, 256, False, False)
-        mx(0, 1, 1, 1, 1, "C", 512, 512, 0, False, True)
-        ev(0, 1, 1)
-        mx(0, 1, 2, 2, 0, "F", 0, 128, 128, False, False)
-        mx(0, 1, 2, 2, 0, "F", 128, 256, 256, False, False)
-        mx(0, 1, 2, 2, 1, "F", 384, 128, 128, False, False)
-        mx(0, 1, 2, 2, 1, "F", 512, 256, 256, False, False)
-        mx(0, 1, 2, 1, 1, "C", 512, 512, 0, False, True)
-        ev(0, 1, 2)
-        mx(0, 1, 3, 2, 0, "F", 0, 128, 128, False, False)
-        mx(0, 1, 3, 2, 0, "F", 128, 256, 256, False, False)
-        mx(0, 1, 3, 2, 1, "F", 384, 128, 128, False, False)
-        mx(0, 1, 3, 2, 1, "F", 512, 256, 256, False, False)
-        mx(0, 1, 3, 1, 1, "C", 512, 512, 0, False, True)
-        ev(0, 1, 3)
-        st(0, 1, 0, 4)
-        mx(1, 1, 0, 0, 0, "B", 0, 512, 0, True, False)
-        mx(1, 1, 0, 2, 0, "F", 0, 128, 128, False, False)
-        mx(1, 1, 0, 2, 0, "F", 128, 256, 256, False, False)
-        mx(1, 1, 0, 1, 0, "C", 0, 512, 0, False, False)
-        mx(1, 1, 0, 0, 1, "B", 512, 512, 0, False, False)
-        mx(1, 1, 0, 2, 1, "F", 384, 128, 128, False, False)
-        mx(1, 1, 0, 2, 1, "F", 512, 256, 256, False, False)
-        mx(1, 1, 0, 1, 1, "C", 512, 512, 0, False, True)
-        ev(1, 1, 0)
-        mx(1, 1, 1, 0, 0, "B", 0, 512, 0, True, False)
-        mx(1, 1, 1, 2, 0, "F", 0, 128, 128, False, False)
-        mx(1, 1, 1, 2, 0, "F", 128, 256, 256, False, False)
-        mx(1, 1, 1, 1, 0, "C", 0, 512, 0, False, False)
-        mx(1, 1, 1, 0, 1, "B", 512, 512, 0, False, False)
-        mx(1, 1, 1, 2, 1, "F", 384, 128, 128, False, False)
-        mx(1, 1, 1, 2, 1, "F", 512, 256, 256, False, False)
-        mx(1, 1, 1, 1, 1, "C", 512, 512, 0, False, True)
-        ev(1, 1, 1)
-        st(1, 1, 0, 2)
-        mx(1, 1, 2, 0, 0, "B", 0, 512, 0, True, False)
-        mx(1, 1, 2, 2, 0, "F", 0, 128, 128, False, False)
-        mx(1, 1, 2, 2, 0, "F", 128, 256, 256, False, False)
-        mx(1, 1, 2, 1, 0, "C", 0, 512, 0, False, False)
-        mx(1, 1, 2, 0, 1, "B", 512, 512, 0, False, False)
-        mx(1, 1, 2, 2, 1, "F", 384, 128, 128, False, False)
-        mx(1, 1, 2, 2, 1, "F", 512, 256, 256, False, False)
-        mx(1, 1, 2, 1, 1, "C", 512, 512, 0, False, True)
-        ev(1, 1, 2)
-        st(1, 1, 2, 3)
-        mx(1, 2, 3, 0, 0, "B", 0, 256, 0, True, False)
-        mx(1, 2, 3, 2, 0, "F", 0, 128, 128, False, False)
-        mx(1, 2, 3, 1, 0, "C", 0, 256, 0, False, False)
-        mx(1, 2, 3, 0, 1, "B", 512, 256, 0, False, False)
-        mx(1, 2, 3, 2, 1, "F", 384, 128, 128, False, False)
-        mx(1, 2, 3, 1, 1, "C", 512, 256, 0, False, True)
-        ev(1, 2, 3)
-        st(1, 2, 3, 4)
-        mx(1, 3, 3, 0, 0, "B", 256, 256, 256, True, False)
-        mx(1, 3, 3, 2, 0, "F", 128, 256, 256, False, False)
-        mx(1, 3, 3, 1, 0, "C", 256, 256, 256, False, False)
-        mx(1, 3, 3, 0, 1, "B", 768, 256, 256, False, False)
-        mx(1, 3, 3, 2, 1, "F", 512, 256, 256, False, False)
-        mx(1, 3, 3, 1, 1, "C", 768, 256, 256, False, True)
-        ev(1, 3, 3)
-        st(1, 3, 3, 4)
+
+        flip("now_lo", range(4))
+        copy_out("now_lo", range(4), ["scalar", "vector", "scalar", "vector"])
+        flip("x0", [0, 1])
+        quantise("now_lo", 0, 2048)
+        copy_out("x0", [0, 1], ["scalar", "vector"])
+        quantise("now_lo", 2048, 4096)
+        flip("x0", [2, 3])
+        quantise("x0", 0, 2048)
+        copy_out("x0", [2, 3], ["scalar", "vector"])
+        flip("back1_lo", [0])
+        copy_out("back1_lo", [0], ["scalar"])
+        flip("x1", [0, 1])
+        quantise("x0", 2048, 4096)
+        move(0, 3)
+        quantise("back1_lo", 0, 1024)
+        quantise("moved0", 1024, 2048)
+
+        for r in range(R):
+            passes(0, "low", r, [(0, 0)], begin=True)
+        copy_out("x1", [0, 1], ["scalar", "scalar"])
+        flip("x1", [2, 3])
+        copy_out("x1", [2, 3], ["scalar", "scalar"])
+        for r in (1, 2, 3, 0):
+            passes(0, "low", r, [(1, 0), (1, 1), (0, 1)], end=True)
+        quantise("x1", 0, 2048)
+        leave(0, "low", 1)
+        quantise("x1", 2048, 4096)
+        move(1, 3)
+        quantise("moved1", 1024, 2048)
+        for r in (2, 3, 0):
+            leave(0, "low", r)
+        store(0, "low", 0, R)
+
+        flip("now_hi", range(4))
+        copy_out("now_hi", range(4), ["scalar"] * 4)
+        for r in range(R):
+            passes(1, "low", r, [(0, 0)], begin=True)
+        flip("back1_hi", range(4))
+        copy_out("back1_hi", range(4), ["scalar"] * 4)
+        for r in (1, 2, 3, 0):
+            passes(1, "low", r, [(1, 0), (1, 1), (0, 1)], end=True)
+        quantise("now_hi", 0, 2048)
+        quantise("now_hi", 2048, 4096)
+        for r in (1, 2, 3, 0):
+            leave(1, "low", r)
+        store(1, "low", 0, R)
+
+        flip("back2", range(3))
+        copy_out("back2", range(3), ["scalar"] * 3)
+        move(0, 2)
+        quantise("moved0", 0, 1024)
+        for r in range(R):
+            passes(0, "high", r, [(0, 0), (0, 1)], begin=True)
+        quantise("back1_hi", 0, 2048)
+        quantise("back1_hi", 2048, 4096)
+        for r in range(R):
+            passes(0, "high", r, [(1, 0)])
+        quantise("back2", 0, 2048)
+        quantise("back2", 2048, 3072)
+        move(1, 2)
+        quantise("moved1", 0, 1024)
+        for r in range(R):
+            passes(0, "high", r, [(2, 0), (2, 1), (1, 1)], end=True)
+            leave(0, "high", r)
+        store(0, "high", 0, R)
+
+        for r0, r1 in ((0, 2), (2, 3)):
+            for r in range(r0, r1):
+                passes(1, "high", r, HIGH_AT_ONCE, begin=True, end=True)
+                leave(1, "high", r)
+            store(1, "high", r0, r1)
+        for kind in ("high_left", "high_right"):
+            passes(1, kind, 3, HIGH_AT_ONCE, begin=True, end=True)
+            leave(1, kind, 3)
+            store(1, kind, 3, R)

@@ -175,6 +175,17 @@ def tile_multiheadhomogeneousattention_pa_kernel(tc, x, w_now, w_back1, w_back2,
             )
 
 
+        def low(n):
+            for r in range(R):
+                passes(n, "low", r, [(0, 0), (0, 1)], begin=True)
+            for r in (1, 2, 3, 0):
+                passes(n, "low", r, [(1, 0), (1, 1)], end=True)
+
+        def leave_low(n):
+            for r in (1, 2, 3, 0):
+                leave(n, "low", r)
+            store(n, "low", 0, R)
+
         flip("now_lo", range(4))
         copy_out("now_lo", range(4), ["scalar", "vector", "scalar", "vector"])
         flip("x0", [0, 1])
@@ -187,45 +198,36 @@ def tile_multiheadhomogeneousattention_pa_kernel(tc, x, w_now, w_back1, w_back2,
         flip("back1_lo", [0])
         copy_out("back1_lo", [0], ["scalar"])
         flip("x1", [0, 1])
+        copy_out("x1", [0, 1], ["scalar", "scalar"])
         quantise("x0", 2048, 4096)
         move(0, 3)
         quantise("back1_lo", 0, 1024)
         quantise("moved0", 1024, 2048)
+        quantise("x1", 0, 2048)
 
-        for r in range(R):
-            passes(0, "low", r, [(0, 0)], begin=True)
-        copy_out("x1", [0, 1], ["scalar", "scalar"])
+        low(0)
+        leave_low(0)
+
         flip("x1", [2, 3])
         copy_out("x1", [2, 3], ["scalar", "scalar"])
-        for r in (1, 2, 3, 0):
-            passes(0, "low", r, [(1, 0), (1, 1), (0, 1)], end=True)
-        quantise("x1", 0, 2048)
-        leave(0, "low", 1)
         quantise("x1", 2048, 4096)
         move(1, 3)
         quantise("moved1", 1024, 2048)
-        for r in (2, 3, 0):
-            leave(0, "low", r)
-        store(0, "low", 0, R)
-
         flip("now_hi", range(4))
         copy_out("now_hi", range(4), ["scalar"] * 4)
-        for r in range(R):
-            passes(1, "low", r, [(0, 0)], begin=True)
-        flip("back1_hi", range(4))
-        copy_out("back1_hi", range(4), ["scalar"] * 4)
-        for r in (1, 2, 3, 0):
-            passes(1, "low", r, [(1, 0), (1, 1), (0, 1)], end=True)
         quantise("now_hi", 0, 2048)
         quantise("now_hi", 2048, 4096)
-        for r in (1, 2, 3, 0):
-            leave(1, "low", r)
-        store(1, "low", 0, R)
 
+        low(1)
+        leave_low(1)
+
+        flip("back1_hi", range(4))
+        copy_out("back1_hi", range(4), ["scalar"] * 4)
         flip("back2", range(3))
         copy_out("back2", range(3), ["scalar"] * 3)
         move(0, 2)
         quantise("moved0", 0, 1024)
+
         for r in range(R):
             passes(0, "high", r, [(0, 0), (0, 1)], begin=True)
         quantise("back1_hi", 0, 2048)

@@ -15,9 +15,9 @@ G = D // (4 * P)
 BANK = 512
 FLOPS = 2 * B * S * D * P * (8 + 5 + 3)
 
-WEIGHT_TILES = {"now_lo": 4, "back1_lo": 1, "now_hi": 4, "back1_hi": 4, "back2": 3}
+WEIGHT_PANELS = {"now_lo": 4, "back1_lo": 1, "now_hi": 4, "back1_hi": 4, "back2": 3}
 
-BANKS = {
+ACCUMULATORS = {
     "low": (0, 4, {0: [("now_lo", 0, 4, 0)], 1: [("back1_lo", 0, 1, 3)]}),
     "high": (4, 4, {0: [("now_hi", 0, 4, 4)], 1: [("back1_hi", 0, 4, 4)], 2: [("back2", 0, 1, 5), ("back2", 1, 2, 6)]}),
     "high_left": (4, 2, {0: [("now_hi", 0, 2, 4)], 1: [("back1_hi", 0, 2, 4)], 2: [("back2", 0, 1, 5)]}),
@@ -37,14 +37,14 @@ def tile_multiheadhomogeneousattention_pa_kernel(tc, x, w_now, w_back1, w_back2,
         psum = ctx.enter_context(tc.psum_pool(name="psum", bufs=8))
         ctx.enter_context(tc.manual_schedule())
 
-        tiles_of = dict(WEIGHT_TILES)
+        panels_of = dict(WEIGHT_PANELS)
         moved = ["moved%d" % n for n in range(B)]
         for n in range(B):
-            tiles_of["x%d" % n] = R
-            tiles_of[moved[n]] = 2
+            panels_of["x%d" % n] = R
+            panels_of[moved[n]] = 2
         raw, grouped, words, scales = {}, {}, {}, {}
-        for name in sorted(tiles_of):
-            cols = tiles_of[name] * D
+        for name in sorted(panels_of):
+            cols = panels_of[name] * D
             if name not in moved:
                 raw[name] = raw_pool.tile([P, cols], BF16, name="raw_" + name)
             grouped[name] = grouped_pool.tile([P, cols], BF16, name="grouped_" + name, align_bytes=64)
@@ -89,8 +89,8 @@ def tile_multiheadhomogeneousattention_pa_kernel(tc, x, w_now, w_back1, w_back2,
         make_identity(nc, identity[:])
         nc.vector.memset(ones[:], 1.0)
         nc.vector.memset(bias_row[:], 0.0)
-        for n in range(B):
-            nc.vector.memset(grouped["moved%d" % n][:].bitcast(F32), 0.0)
+        for name in moved:
+            nc.vector.memset(grouped[name][:].bitcast(F32), 0.0)
         nc.vector.tensor_copy(out=bias_row[0:1, :], in_=bias_in[:])
         for half in range(2):
             spread = psum.tile([P, BANK], F32, name="spread", tag="bank")
@@ -101,32 +101,35 @@ def tile_multiheadhomogeneousattention_pa_kernel(tc, x, w_now, w_back1, w_back2,
         flipped = {}
         acc = {}
 
+        def every(name):
+            return range(panels_of[name])
+
         def word_column(name, t, g):
-            if name in WEIGHT_TILES:
-                return (g * tiles_of[name] + t) * P
+            if name in WEIGHT_PANELS:
+                return (g * panels_of[name] + t) * P
             return (t * G + g) * P
 
-        def flip(name, tiles):
-            for t in tiles:
+        def flip(name, panels):
+            for t in panels:
                 bank = psum.tile([P, BANK], F32, name="bank", tag="bank")
                 for c in range(4):
                     first = t * BANK + c * P
                     nc.tensor.transpose(bank[:, c * P:(c + 1) * P], raw[name][:].bitcast(F32)[:, first:first + P], identity[:])
                 flipped[(name, t)] = bank
 
-        def copy_out(name, tiles, engines):
-            order = "q (g t m u) -> q g t m u" if name in WEIGHT_TILES else "q (t g m u) -> q g t m u"
-            dst = grouped[name][:].bitcast(F32).rearrange(order, g=G, t=tiles_of[name], u=2)
-            for t, engine in zip(tiles, engines):
+        def copy_out(name, panels, share=False):
+            order = "q (g t m u) -> q g t m u" if name in WEIGHT_PANELS else "q (t g m u) -> q g t m u"
+            dst = grouped[name][:].bitcast(F32).rearrange(order, g=G, t=panels_of[name], u=2)
+            for t in panels:
                 src = flipped[(name, t)][:].rearrange("q (g u m) -> q g m u", g=G, u=2)
-                if engine == "vector":
+                if share and t % 2 == 1:
                     nc.vector.tensor_copy(out=dst[:, :, t, :, :], in_=src)
                 else:
                     nc.scalar.copy(out=dst[:, :, t, :, :], in_=src)
 
         def move(n, r):
             nc.vector.tensor_copy(
-                out=grouped["moved%d" % n][:].rearrange("q (t g c) -> q t g c", t=2, g=G)[:, r - 2, :, 4:4 * P],
+                out=grouped[moved[n]][:].rearrange("q (t g c) -> q t g c", t=2, g=G)[:, r - 2, :, 4:4 * P],
                 in_=grouped["x%d" % n][:].rearrange("q (t g c) -> q t g c", t=R, g=G)[:, r, :, 0:4 * P - 4],
             )
 
@@ -140,9 +143,9 @@ def tile_multiheadhomogeneousattention_pa_kernel(tc, x, w_now, w_back1, w_back2,
         def passes(n, kind, r, todo, begin=False, end=False):
             if begin:
                 acc[(n, kind, r)] = psum.tile([P, BANK], F32, name="acc", tag="bank")
-            pieces = [(tap, g, piece) for tap, g in todo for piece in BANKS[kind][2][tap]]
+            pieces = [(tap, g, piece) for tap, g in todo for piece in ACCUMULATORS[kind][2][tap]]
             for i, (tap, g, (name, t0, count, head)) in enumerate(pieces):
-                tokens, t = ("x%d" % n, r - tap) if r >= tap else ("moved%d" % n, r - tap + 2)
+                tokens, t = ("x%d" % n, r - tap) if r >= tap else (moved[n], r - tap + 2)
                 a = word_column(tokens, t, g)
                 b = word_column(name, t0, g)
                 o = (head % 4) * P
@@ -156,8 +159,8 @@ def tile_multiheadhomogeneousattention_pa_kernel(tc, x, w_now, w_back1, w_back2,
                     stop=end and i == len(pieces) - 1,
                 )
 
-        def leave(n, kind, r):
-            head, count = BANKS[kind][0], BANKS[kind][1]
+        def finish(n, kind, r):
+            head, count = ACCUMULATORS[kind][0], ACCUMULATORS[kind][1]
             h0 = head % 4
             nc.vector.tensor_tensor(
                 out=y_sb[(n, head // 4)][:].rearrange("q (h r p) -> q h r p", h=4, r=R)[:, h0:h0 + count, r, :],
@@ -167,88 +170,90 @@ def tile_multiheadhomogeneousattention_pa_kernel(tc, x, w_now, w_back1, w_back2,
             )
 
         def store(n, kind, r0, r1):
-            head, count = BANKS[kind][0], BANKS[kind][1]
+            head, count = ACCUMULATORS[kind][0], ACCUMULATORS[kind][1]
             h0 = head % 4
             nc.sync.dma_start(
                 out=out[n, head:head + count].rearrange("h (m r) p -> m h r p", r=R)[:, :, r0:r1, :],
                 in_=y_sb[(n, head // 4)][:].rearrange("q (h r p) -> q h r p", h=4, r=R)[:, h0:h0 + count, r0:r1, :],
             )
 
-
-        def low(n):
+        def open_low(n):
             for r in range(R):
-                passes(n, "low", r, [(0, 0), (0, 1)], begin=True)
-            for r in (1, 2, 3, 0):
-                passes(n, "low", r, [(1, 0), (1, 1)], end=True)
+                passes(n, "low", r, [(0, 0)], begin=True)
 
-        def leave_low(n):
+        def close_low(n):
             for r in (1, 2, 3, 0):
-                leave(n, "low", r)
-            store(n, "low", 0, R)
+                passes(n, "low", r, [(1, 0), (1, 1), (0, 1)], end=True)
 
-        flip("now_lo", range(4))
-        copy_out("now_lo", range(4), ["scalar", "vector", "scalar", "vector"])
+
+        flip("now_lo", every("now_lo"))
+        copy_out("now_lo", every("now_lo"), share=True)
         flip("x0", [0, 1])
-        quantise("now_lo", 0, 2048)
-        copy_out("x0", [0, 1], ["scalar", "vector"])
-        quantise("now_lo", 2048, 4096)
+        quantise("now_lo", 0, 2 * D)
+        copy_out("x0", [0, 1], share=True)
+        quantise("now_lo", 2 * D, 4 * D)
         flip("x0", [2, 3])
-        quantise("x0", 0, 2048)
-        copy_out("x0", [2, 3], ["scalar", "vector"])
-        flip("back1_lo", [0])
-        copy_out("back1_lo", [0], ["scalar"])
+        quantise("x0", 0, 2 * D)
+        copy_out("x0", [2, 3], share=True)
+        flip("back1_lo", every("back1_lo"))
+        copy_out("back1_lo", every("back1_lo"))
         flip("x1", [0, 1])
-        copy_out("x1", [0, 1], ["scalar", "scalar"])
-        quantise("x0", 2048, 4096)
+        quantise("x0", 2 * D, 4 * D)
         move(0, 3)
-        quantise("back1_lo", 0, 1024)
-        quantise("moved0", 1024, 2048)
-        quantise("x1", 0, 2048)
+        quantise("back1_lo", 0, D)
+        quantise("moved0", D, 2 * D)
 
-        low(0)
-        leave_low(0)
-
+        open_low(0)
+        copy_out("x1", [0, 1])
         flip("x1", [2, 3])
-        copy_out("x1", [2, 3], ["scalar", "scalar"])
-        quantise("x1", 2048, 4096)
+        copy_out("x1", [2, 3])
+        close_low(0)
+        quantise("x1", 0, 2 * D)
+        finish(0, "low", 1)
+        quantise("x1", 2 * D, 4 * D)
         move(1, 3)
-        quantise("moved1", 1024, 2048)
-        flip("now_hi", range(4))
-        copy_out("now_hi", range(4), ["scalar"] * 4)
-        quantise("now_hi", 0, 2048)
-        quantise("now_hi", 2048, 4096)
+        quantise("moved1", D, 2 * D)
+        for r in (2, 3, 0):
+            finish(0, "low", r)
+        store(0, "low", 0, R)
 
-        low(1)
-        leave_low(1)
+        flip("now_hi", every("now_hi"))
+        copy_out("now_hi", every("now_hi"))
+        open_low(1)
+        close_low(1)
+        quantise("now_hi", 0, 2 * D)
+        quantise("now_hi", 2 * D, 4 * D)
+        for r in (1, 2, 3, 0):
+            finish(1, "low", r)
+        store(1, "low", 0, R)
 
-        flip("back1_hi", range(4))
-        copy_out("back1_hi", range(4), ["scalar"] * 4)
-        flip("back2", range(3))
-        copy_out("back2", range(3), ["scalar"] * 3)
+        flip("back1_hi", every("back1_hi"))
+        copy_out("back1_hi", every("back1_hi"))
+        flip("back2", every("back2"))
+        copy_out("back2", every("back2"))
         move(0, 2)
-        quantise("moved0", 0, 1024)
-
+        quantise("moved0", 0, D)
         for r in range(R):
             passes(0, "high", r, [(0, 0), (0, 1)], begin=True)
-        quantise("back1_hi", 0, 2048)
-        quantise("back1_hi", 2048, 4096)
+        quantise("back1_hi", 0, 2 * D)
+        quantise("back1_hi", 2 * D, 4 * D)
         for r in range(R):
             passes(0, "high", r, [(1, 0)])
-        quantise("back2", 0, 2048)
-        quantise("back2", 2048, 3072)
+        quantise("back2", 0, 2 * D)
+        quantise("back2", 2 * D, 3 * D)
         move(1, 2)
-        quantise("moved1", 0, 1024)
+        quantise("moved1", 0, D)
         for r in range(R):
             passes(0, "high", r, [(2, 0), (2, 1), (1, 1)], end=True)
-            leave(0, "high", r)
+            finish(0, "high", r)
         store(0, "high", 0, R)
 
         for r0, r1 in ((0, 2), (2, 3)):
             for r in range(r0, r1):
                 passes(1, "high", r, HIGH_AT_ONCE, begin=True, end=True)
-                leave(1, "high", r)
+                finish(1, "high", r)
             store(1, "high", r0, r1)
         for kind in ("high_left", "high_right"):
             passes(1, kind, 3, HIGH_AT_ONCE, begin=True, end=True)
-            leave(1, kind, 3)
+            finish(1, kind, 3)
             store(1, kind, 3, R)

from contextlib import ExitStack

import concourse.mybir as mybir
from concourse.masks import make_identity

F32 = mybir.dt.float32
BF16 = mybir.dt.bfloat16
U32 = mybir.dt.uint32
U8 = mybir.dt.uint8
FP8X4 = mybir.dt.float8_e4m3fn_x4

B, S, D, P, H = 2, 512, 1024, 128, 8
R = S // P
G = D // (4 * P)
BANK = 512
FLOPS = 2 * B * S * D * P * (8 + 5 + 3)

WEIGHT_PANELS = {"now_lo": 4, "back1_lo": 1, "now_hi": 4, "back1_hi": 4, "back2": 3}

ACCUMULATORS = {
    "low": (0, 4, {0: [("now_lo", 0, 4, 0)], 1: [("back1_lo", 0, 1, 3)]}),
    "high": (4, 4, {0: [("now_hi", 0, 4, 4)], 1: [("back1_hi", 0, 4, 4)], 2: [("back2", 0, 1, 5), ("back2", 1, 2, 6)]}),
    "high_left": (4, 2, {0: [("now_hi", 0, 2, 4)], 1: [("back1_hi", 0, 2, 4)], 2: [("back2", 0, 1, 5)]}),
    "high_right": (6, 2, {0: [("now_hi", 2, 2, 6)], 1: [("back1_hi", 2, 2, 6)], 2: [("back2", 1, 2, 6)]}),
}
HIGH_AT_ONCE = [(0, 0), (2, 0), (1, 0), (0, 1), (2, 1), (1, 1)]


def tile_multiheadhomogeneousattention_pa_kernel(tc, x, w_now, w_back1, w_back2, bias, out):
    nc = tc.nc
    with ExitStack() as ctx:
        const = ctx.enter_context(tc.tile_pool(name="const", bufs=1))
        raw_pool = ctx.enter_context(tc.tile_pool(name="raw", bufs=1))
        grouped_pool = ctx.enter_context(tc.tile_pool(name="grouped", bufs=1))
        mx_pool = ctx.enter_context(tc.tile_pool(name="mx", bufs=1))
        out_pool = ctx.enter_context(tc.tile_pool(name="outp", bufs=1))
        psum = ctx.enter_context(tc.psum_pool(name="psum", bufs=8))
        ctx.enter_context(tc.manual_schedule())

        panels_of = dict(WEIGHT_PANELS)
        moved = ["moved%d" % n for n in range(B)]
        for n in range(B):
            panels_of["x%d" % n] = R
            panels_of[moved[n]] = 2
        raw, grouped, words, scales = {}, {}, {}, {}
        for name in sorted(panels_of):
            cols = panels_of[name] * D
            if name not in moved:
                raw[name] = raw_pool.tile([P, cols], BF16, name="raw_" + name)
            grouped[name] = grouped_pool.tile([P, cols], BF16, name="grouped_" + name, align_bytes=64)
            words[name] = mx_pool.tile([P, cols // 4], U32, name="words_" + name, align_bytes=64)
            scales[name] = mx_pool.tile([P, cols // 4], U8, name="scales_" + name, align_bytes=64)
        y_sb = {}
        for n in range(B):
            for half in range(2):
                y_sb[(n, half)] = out_pool.tile([P, 4 * R * P], F32, name="y_sb%d%d" % (n, half))
        identity = const.tile([P, P], F32, name="identity")
        ones = const.tile([P, P], BF16, name="ones")
        bias_in = const.tile([1, H * P], BF16, name="bias_in")
        bias_row = const.tile([P, H * P], BF16, name="bias_row")
        bias_all = const.tile([P, H * P], F32, name="bias_all")

        def load_w(name, src, t0, t1):
            nc.sync.dma_start(
                out=raw[name][:, t0 * D:t1 * D].rearrange("p (t d) -> p t d", t=t1 - t0),
                in_=src[t0:t1].rearrange("t p d -> p t d"),
            )

        def load_x(n, r0, r1):
            nc.sync.dma_start(
                out=raw["x%d" % n][:, r0 * D:r1 * D],
                in_=x[n].rearrange("(m r) d -> m (r d)", r=R)[:, r0 * D:r1 * D],
            )

        nc.sync.dma_start(out=bias_in[:], in_=bias.rearrange("(o h) p -> o (h p)", o=1))
        load_w("now_lo", w_now[0:4], 0, 2)
        load_w("now_lo", w_now[0:4], 2, 4)
        load_x(0, 0, 2)
        load_x(0, 2, 4)
        load_w("back1_lo", w_back1[0:1], 0, 1)
        load_x(1, 0, 2)
        load_x(1, 2, 4)
        load_w("now_hi", w_now[4:8], 0, 2)
        load_w("now_hi", w_now[4:8], 2, 4)
        load_w("back1_hi", w_back1[1:5], 0, 2)
        load_w("back1_hi", w_back1[1:5], 2, 4)
        load_w("back2", w_back2, 0, 3)

        make_identity(nc, identity[:])
        nc.vector.memset(ones[:], 1.0)
        nc.vector.memset(bias_row[:], 0.0)
        for name in moved:
            nc.vector.memset(grouped[name][:].bitcast(F32), 0.0)
        nc.vector.tensor_copy(out=bias_row[0:1, :], in_=bias_in[:])
        for half in range(2):
            spread = psum.tile([P, BANK], F32, name="spread", tag="bank")
            cols = slice(half * BANK, (half + 1) * BANK)
            nc.tensor.matmul(spread[:], lhsT=ones[:], rhs=bias_row[:, cols], start=True, stop=True)
            nc.scalar.copy(out=bias_all[:, cols], in_=spread[:])

        flipped = {}
        acc = {}

        def every(name):
            return range(panels_of[name])

        def word_column(name, t, g):
            if name in WEIGHT_PANELS:
                return (g * panels_of[name] + t) * P
            return (t * G + g) * P

        def flip(name, panels):
            for t in panels:
                bank = psum.tile([P, BANK], F32, name="bank", tag="bank")
                for c in range(4):
                    first = t * BANK + c * P
                    nc.tensor.transpose(bank[:, c * P:(c + 1) * P], raw[name][:].bitcast(F32)[:, first:first + P], identity[:])
                flipped[(name, t)] = bank

        def copy_out(name, panels, share=False):
            order = "q (g t m u) -> q g t m u" if name in WEIGHT_PANELS else "q (t g m u) -> q g t m u"
            dst = grouped[name][:].bitcast(F32).rearrange(order, g=G, t=panels_of[name], u=2)
            for t in panels:
                src = flipped[(name, t)][:].rearrange("q (g u m) -> q g m u", g=G, u=2)
                if share and t % 2 == 1:
                    nc.vector.tensor_copy(out=dst[:, :, t, :, :], in_=src)
                else:
                    nc.scalar.copy(out=dst[:, :, t, :, :], in_=src)

        def move(n, r):
            nc.vector.tensor_copy(
                out=grouped[moved[n]][:].rearrange("q (t g c) -> q t g c", t=2, g=G)[:, r - 2, :, 4:4 * P],
                in_=grouped["x%d" % n][:].rearrange("q (t g c) -> q t g c", t=R, g=G)[:, r, :, 0:4 * P - 4],
            )

        def quantise(name, c0, c1):
            nc.vector.quantize_mx(
                out=words[name][:, c0 // 4:c1 // 4].bitcast(FP8X4),
                scales=scales[name][:, c0 // 4:c1 // 4],
                in_=grouped[name][:, c0:c1],
            )

        def passes(n, kind, r, todo, begin=False, end=False):
            if begin:
                acc[(n, kind, r)] = psum.tile([P, BANK], F32, name="acc", tag="bank")
            pieces = [(tap, g, piece) for tap, g in todo for piece in ACCUMULATORS[kind][2][tap]]
            for i, (tap, g, (name, t0, count, head)) in enumerate(pieces):
                tokens, t = ("x%d" % n, r - tap) if r >= tap else (moved[n], r - tap + 2)
                a = word_column(tokens, t, g)
                b = word_column(name, t0, g)
                o = (head % 4) * P
                nc.tensor.matmul_mx(
                    out=acc[(n, kind, r)][:, o:o + count * P],
                    lhsT=words[tokens][:, a:a + P].bitcast(FP8X4),
                    lhsT_scale=scales[tokens][:, a:a + P],
                    rhs=words[name][:, b:b + count * P].bitcast(FP8X4),
                    rhs_scale=scales[name][:, b:b + count * P],
                    start=begin and i == 0,
                    stop=end and i == len(pieces) - 1,
                )

        def finish(n, kind, r):
            head, count = ACCUMULATORS[kind][0], ACCUMULATORS[kind][1]
            h0 = head % 4
            nc.vector.tensor_tensor(
                out=y_sb[(n, head // 4)][:].rearrange("q (h r p) -> q h r p", h=4, r=R)[:, h0:h0 + count, r, :],
                in0=acc[(n, kind, r)][:, h0 * P:(h0 + count) * P].rearrange("q (h p) -> q h p", h=count),
                in1=bias_all[:, head * P:(head + count) * P].rearrange("q (h p) -> q h p", h=count),
                op=mybir.AluOpType.add,
            )

        def store(n, kind, r0, r1):
            head, count = ACCUMULATORS[kind][0], ACCUMULATORS[kind][1]
            h0 = head % 4
            nc.sync.dma_start(
                out=out[n, head:head + count].rearrange("h (m r) p -> m h r p", r=R)[:, :, r0:r1, :],
                in_=y_sb[(n, head // 4)][:].rearrange("q (h r p) -> q h r p", h=4, r=R)[:, h0:h0 + count, r0:r1, :],
            )

        def open_low(n):
            for r in range(R):
                passes(n, "low", r, [(0, 0)], begin=True)

        def close_low(n):
            for r in (1, 2, 3, 0):
                passes(n, "low", r, [(1, 0), (1, 1), (0, 1)], end=True)


        flip("now_lo", every("now_lo"))
        copy_out("now_lo", every("now_lo"), share=True)
        flip("x0", [0, 1])
        quantise("now_lo", 0, 2 * D)
        copy_out("x0", [0, 1], share=True)
        quantise("now_lo", 2 * D, 4 * D)
        flip("x0", [2, 3])
        quantise("x0", 0, 2 * D)
        copy_out("x0", [2, 3], share=True)
        flip("back1_lo", every("back1_lo"))
        copy_out("back1_lo", every("back1_lo"))
        flip("x1", [0, 1])
        quantise("x0", 2 * D, 4 * D)
        move(0, 3)
        quantise("back1_lo", 0, D)
        quantise("moved0", D, 2 * D)

        open_low(0)
        copy_out("x1", [0, 1])
        flip("x1", [2, 3])
        copy_out("x1", [2, 3])
        close_low(0)
        quantise("x1", 0, 2 * D)
        finish(0, "low", 1)
        quantise("x1", 2 * D, 4 * D)
        move(1, 3)
        quantise("moved1", D, 2 * D)
        for r in (2, 3, 0):
            finish(0, "low", r)
        store(0, "low", 0, R)

        flip("now_hi", every("now_hi"))
        copy_out("now_hi", every("now_hi"))
        open_low(1)
        close_low(1)
        quantise("now_hi", 0, 2 * D)
        quantise("now_hi", 2 * D, 4 * D)
        for r in (1, 2, 3, 0):
            finish(1, "low", r)
        store(1, "low", 0, R)

        flip("back1_hi", every("back1_hi"))
        copy_out("back1_hi", every("back1_hi"))
        flip("back2", every("back2"))
        copy_out("back2", every("back2"))
        move(0, 2)
        quantise("moved0", 0, D)
        for r in range(R):
            passes(0, "high", r, [(0, 0), (0, 1)], begin=True)
        quantise("back1_hi", 0, 2 * D)
        quantise("back1_hi", 2 * D, 4 * D)
        for r in range(R):
            passes(0, "high", r, [(1, 0)])
        quantise("back2", 0, 2 * D)
        quantise("back2", 2 * D, 3 * D)
        move(1, 2)
        quantise("moved1", 0, D)
        for r in range(R):
            passes(0, "high", r, [(2, 0), (2, 1), (1, 1)], end=True)
            finish(0, "high", r)
        store(0, "high", 0, R)

        for r0, r1 in ((0, 2), (2, 3)):
            for r in range(r0, r1):
                passes(1, "high", r, HIGH_AT_ONCE, begin=True, end=True)
                finish(1, "high", r)
            store(1, "high", r0, r1)
        for kind in ("high_left", "high_right"):
            passes(1, kind, 3, HIGH_AT_ONCE, begin=True, end=True)
            finish(1, kind, 3)
            store(1, kind, 3, R)
